import numpy as np
import ml_dtypes


def mxq(x, axis, fmt="e4m3"):
    dtype, down = {"e4m3": (ml_dtypes.float8_e4m3fn, 7), "e5m2": (ml_dtypes.float8_e5m2, 14)}[fmt]
    v = np.moveaxis(np.asarray(x, np.float32).astype(ml_dtypes.bfloat16).astype(np.float64), axis, -1)
    blocks = v.reshape(v.shape[:-1] + (-1, 32))
    amax = np.abs(blocks).max(-1, keepdims=True)
    byte = np.maximum(np.where(amax > 0, np.frexp(amax)[1] - 1 + 127, 0) - down, 1)
    scale = np.exp2(byte - 127.0)
    codes = (blocks / scale).astype(np.float32).astype(dtype).astype(np.float64)
    return np.moveaxis((codes * scale).reshape(v.shape), -1, axis)


WIDE = False


def mx_kscale(k):
    if not WIDE:
        return np.ones(k)
    levels = np.array([10, -10, 5, -5, 0])
    a = np.random.permutation(np.resize(levels, k // 512 * 4)).reshape(k // 512, 4)
    idx = np.arange(k)
    return np.exp2(a[idx // 512, idx % 128 // 32])


BF16 = ml_dtypes.bfloat16


def bf(x):
    return np.asarray(x, np.float32).astype(BF16)


def f64(x):
    return np.asarray(x).astype(np.float64)


B, P, C, HS, NG = 8, 512, 768, 512, 2
GMIN, GMAX = -1.0, 1.0
SKIP = 1.0


def silu(v):
    return v / (1.0 + np.exp(-v))


def rbf(v):
    grid = np.linspace(GMIN, GMAX, NG)
    denom = (GMAX - GMIN) / (NG - 1)
    return np.exp(-np.square((v[..., None] - grid) / denom))


def setup_inputs():
    s = mx_kscale(HS * NG)[::NG]
    u = s / s.max()
    r = np.sqrt(np.log(1.0 / u))
    d = (GMAX - GMIN) / (NG - 1)
    m = (GMAX + d * r) * (r > 0)
    return {"h_mix": bf(np.random.standard_normal((B, C, HS)) * 0.9 * (d / (d + 2.0 * r)) + m),
            "x": bf(np.random.standard_normal((B, P, C))),
            "fc2_spline_w": bf(np.random.standard_normal((P, HS * NG)) * 0.7 / np.sqrt(HS) / np.repeat(u, NG)),
            "fc2_base_w": bf(np.random.standard_normal((P, HS)) / np.sqrt(HS) / (1.0 + m)),
            "fc2_base_b": bf(np.random.standard_normal(P) * 0.1)}


def reference(h_mix, x, fc2_spline_w, fc2_base_w, fc2_base_b):
    h = f64(h_mix)
    basis = rbf(h).reshape(B, C, HS * NG)
    out = mxq(basis, 2, "e4m3") @ mxq(f64(fc2_spline_w).T, 0, "e4m3")
    out = out + (mxq(silu(h), 2, "e4m3") @ mxq(f64(fc2_base_w).T, 0, "e4m3")) + f64(fc2_base_b)
    return np.swapaxes(out, 1, 2) + SKIP * f64(x)

@@ -1,0 +1,294 @@
+from contextlib import ExitStack
+
+import concourse.mybir as mybir
+from concourse.masks import make_identity
+
+F32 = mybir.dt.float32
+BF16 = mybir.dt.bfloat16
+I32 = mybir.dt.int32
+U32 = mybir.dt.uint32
+U8 = mybir.dt.uint8
+FP8X4 = mybir.dt.float8_e4m3fn_x4
+ACT = mybir.ActivationFunctionType
+ALU = mybir.AluOpType
+
+P = 128
+BATCH = 8
+TOKENS = 768
+HIDDEN = 512
+OUTS = 512
+M_TILES = OUTS // P
+PACK = 4
+K_PASS = P * PACK
+PASSES = 3
+HALVES = 2
+CENTRES = 2
+UNIT = 256
+UNITS = BATCH * TOKENS // UNIT
+UNITS_PER_BATCH = TOKENS // UNIT
+UNIT_H = HALVES * UNIT * 2
+WORDS = HIDDEN // 2
+LOADS_AHEAD = 6
+COPIES_AHEAD = 2
+WEIGHT_BANKS = 2 * PASSES
+WEIGHT_EVERY = UNITS // WEIGHT_BANKS
+X_TILES = 3
+
+FLOPS = 2 * BATCH * TOKENS * OUTS * (HIDDEN * CENTRES + HIDDEN)
+
+
+def tile_kan1_pb_t_kernel(tc, h_mix, x, fc2_spline_w, fc2_base_w, fc2_base_b, out):
+    nc = tc.nc
+    with ExitStack() as stack:
+        stack.enter_context(tc.manual_schedule())
+        keep = stack.enter_context(tc.tile_pool(name="keep", bufs=1))
+        h_raw_pool = stack.enter_context(tc.tile_pool(name="h_raw", bufs=LOADS_AHEAD))
+        w_pool = stack.enter_context(tc.tile_pool(name="w", bufs=PASSES))
+        silu_pool = stack.enter_context(tc.tile_pool(name="silu", bufs=3))
+        x_pool = stack.enter_context(tc.tile_pool(name="x", bufs=X_TILES))
+        sq_pool = stack.enter_context(tc.tile_pool(name="sq", bufs=2))
+        basis_pool = stack.enter_context(tc.tile_pool(name="basis", bufs=2))
+        out_pool = stack.enter_context(tc.tile_pool(name="out", bufs=4))
+
+        ident = keep.tile([P, P], F32)
+        make_identity(nc, ident[:])
+        one_half = keep.tile([P, 1], F32)
+        nc.vector.memset(one_half[:], 0.5)
+        bias = keep.tile([P, M_TILES], F32)
+        h_t = keep.tile([P, UNITS * UNIT_H], BF16)
+        h_t_words = h_t[:].bitcast(F32)
+        silu_codes = keep.tile([P, UNITS * UNIT], U32, align_bytes=64)
+        silu_scales = keep.tile([P, UNITS * UNIT], U8, align_bytes=64)
+        w_codes = keep.tile([P, PASSES, OUTS], U32, align_bytes=64)
+        w_scales = keep.tile([P, PASSES, OUTS], U8, align_bytes=64)
+
+        h_rows = h_mix.rearrange("b c j -> (b c) j")
+        h_raw_tiles = {}
+
+        def load_h(n):
+            h_raw = h_raw_pool.tile([P, (UNIT // P) * HIDDEN], BF16, name="h_raw")
+            nc.sync.dma_start(
+                out=h_raw[:].rearrange("r (t j) -> r t j", j=HIDDEN),
+                in_=h_rows[n * UNIT : (n + 1) * UNIT, :].rearrange("(t r) j -> r t j", r=P),
+            )
+            h_raw_tiles[n] = h_raw
+
+        w_raw_tiles = {}
+
+        def load_weights(s):
+            w_raw = w_pool.tile([P, M_TILES * K_PASS], BF16, name="w_raw")
+            if s == 0:
+                columns = fc2_base_w
+            else:
+                columns = fc2_spline_w[:, (s - 1) * K_PASS : s * K_PASS]
+            nc.sync.dma_start(
+                out=w_raw[:].rearrange("r (m k) -> r m k", k=K_PASS),
+                in_=columns.rearrange("(m r) k -> r m k", r=P),
+            )
+            w_raw_tiles[s] = w_raw
+
+        x_tiles = {}
+
+        def load_x(b):
+            x_sb = x_pool.tile([P, M_TILES, TOKENS], BF16, name="x_sb")
+            nc.sync.dma_start(out=x_sb[:], in_=x[b].rearrange("(m p) c -> p m c", p=P))
+            x_tiles[b] = x_sb
+
+        for n in range(LOADS_AHEAD):
+            load_h(n)
+        for s in range(PASSES):
+            load_weights(s)
+        bias_rows = keep.tile([P, P], BF16)
+        nc.vector.memset(bias_rows[:].bitcast(I32), 0)
+        nc.sync.dma_start(out=bias_rows[0:M_TILES, :], in_=fc2_base_b.rearrange("(m p) -> m p", p=P))
+
+        sq_tiles = {}
+        basis_bf_tiles = {}
+        basis_mx_tiles = {}
+
+        def h_of_unit(n):
+            return h_t[:, n * UNIT_H : (n + 1) * UNIT_H]
+
+        def square_centre_0(n):
+            sq = sq_pool.tile([P, CENTRES, UNIT_H], F32, name="sq")
+            nc.scalar.activation(
+                out=sq[:, 0, :], in_=h_of_unit(n), func=ACT.Square, scale=0.5, bias=one_half[:]
+            )
+            sq_tiles[n] = sq
+
+        def square_centre_1(n):
+            sq = sq_tiles[n]
+            nc.vector.tensor_tensor(out=sq[:, 1, :], in0=sq[:, 0, :], in1=h_of_unit(n), op=ALU.subtract)
+
+        def exponentials(n):
+            basis_bf = basis_pool.tile([P, UNIT_H, CENTRES], BF16, name="basis_bf", align_bytes=64)
+            nc.scalar.activation(
+                out=basis_bf[:],
+                in_=sq_tiles[n][:].rearrange("p i c -> p c i"),
+                func=ACT.Exp,
+                scale=-1.0,
+            )
+            basis_bf_tiles[n] = basis_bf
+
+        def quantise_basis(n):
+            basis_codes = basis_pool.tile([P, HALVES * UNIT], U32, name="basis_codes", align_bytes=64)
+            basis_scales = basis_pool.tile([P, HALVES * UNIT], U8, name="basis_scales", align_bytes=64)
+            nc.vector.quantize_mx(
+                out=basis_codes[:].bitcast(FP8X4),
+                scales=basis_scales[:],
+                in_=basis_bf_tiles[n][:].rearrange("p c i -> p (c i)"),
+            )
+            basis_mx_tiles[n] = (basis_codes, basis_scales)
+
+        with tc.psum_pool(name="h_bank", bufs=4) as h_psum, tc.psum_pool(name="w_bank", bufs=2) as w_psum:
+            silu_bf_tiles = {}
+            w_bf_tiles = {}
+
+            def transpose_h(n):
+                h_words = h_raw_tiles[n][:].bitcast(F32)
+                h_bank = h_psum.tile([P, HALVES * UNIT], F32, name="h_bank")
+                for t in range(UNIT // P):
+                    for u in range(HALVES):
+                        nc.tensor.transpose(
+                            h_bank[:, u * UNIT + t * P : u * UNIT + (t + 1) * P],
+                            h_words[:, t * WORDS + u * P : t * WORDS + (u + 1) * P],
+                            ident[:],
+                        )
+                nc.vector.tensor_copy(
+                    out=h_t_words[:, n * HALVES * UNIT : (n + 1) * HALVES * UNIT], in_=h_bank[:]
+                )
+
+            def silu(n):
+                silu_bf = silu_pool.tile([P, UNIT_H], BF16, name="silu_bf", align_bytes=64)
+                nc.scalar.activation(
+                    out=silu_bf[:].rearrange("p (w u e) -> p w u e", u=HALVES, e=2),
+                    in_=h_of_unit(n).rearrange("p (u w e) -> p w u e", u=HALVES, e=2),
+                    func=ACT.Silu,
+                )
+                silu_bf_tiles[n] = silu_bf
+
+            def quantise_silu(n):
+                tokens = slice(n * UNIT, (n + 1) * UNIT)
+                nc.vector.quantize_mx(
+                    out=silu_codes[:, tokens].bitcast(FP8X4),
+                    scales=silu_scales[:, tokens],
+                    in_=silu_bf_tiles[n][:],
+                )
+
+            def weight_words(s, m, half):
+                words = w_raw_tiles[s][:].bitcast(F32)
+                first = m * (K_PASS // 2)
+                if s == 0:
+                    return words[:, first + half * P : first + (half + 1) * P]
+                return words[:, first + half : first + 2 * P : 2]
+
+            def transpose_weights(lot):
+                s, pair = divmod(lot, 2)
+                if pair == 0:
+                    w_bf_tiles[s] = w_pool.tile([P, OUTS * PACK], BF16, name="w_bf", align_bytes=64)
+                w_bank = w_psum.tile([P, 2, 2, P], F32, name="w_bank")
+                for i in range(2):
+                    for half in range(2):
+                        nc.tensor.transpose(
+                            w_bank[:, i, half, :], weight_words(s, 2 * pair + i, half), ident[:]
+                        )
+                w_bf_words = w_bf_tiles[s][:].bitcast(F32)
+                nc.vector.tensor_copy(
+                    out=w_bf_words[:, 2 * pair * 2 * P : 2 * (pair + 1) * 2 * P].rearrange(
+                        "p (i r half) -> p i r half", i=2, half=2
+                    ),
+                    in_=w_bank[:].rearrange("p i half r -> p i r half"),
+                )
+
+            def quantise_weights(s):
+                nc.vector.quantize_mx(
+                    out=w_codes[:, s, :].bitcast(FP8X4), scales=w_scales[:, s, :], in_=w_bf_tiles[s][:]
+                )
+
+            def transpose_bias():
+                bias_rows_f32 = keep.tile([P, P], F32)
+                nc.vector.tensor_copy(out=bias_rows_f32[:], in_=bias_rows[:])
+                bias_bank = w_psum.tile([P, P], F32, name="bias_bank", tag="w_bank")
+                nc.tensor.transpose(bias_bank[:], bias_rows_f32[:], ident[:])
+                nc.vector.tensor_copy(out=bias[:], in_=bias_bank[:, 0:M_TILES])
+
+            for n in range(COPIES_AHEAD):
+                transpose_h(n)
+            for n in range(UNITS):
+                if n + LOADS_AHEAD < UNITS:
+                    load_h(n + LOADS_AHEAD)
+                if n + COPIES_AHEAD < UNITS:
+                    transpose_h(n + COPIES_AHEAD)
+                silu(n)
+                if n > 0:
+                    quantise_silu(n - 1)
+                if n % WEIGHT_EVERY == WEIGHT_EVERY - 1:
+                    transpose_weights(n // WEIGHT_EVERY)
+            for b in range(X_TILES):
+                load_x(b)
+            square_centre_0(0)
+            square_centre_1(0)
+            quantise_silu(UNITS - 1)
+            for s in range(PASSES):
+                quantise_weights(s)
+            transpose_bias()
+
+        with tc.psum_pool(name="acc", bufs=8) as acc_psum:
+            acc_tiles = {}
+
+            def matmuls(n):
+                basis_codes, basis_scales = basis_mx_tiles[n]
+                tokens = slice(n * UNIT, (n + 1) * UNIT)
+                moving = [(silu_codes[:, tokens], silu_scales[:, tokens])]
+                for u in range(HALVES):
+                    words = slice(u * UNIT, (u + 1) * UNIT)
+                    moving.append((basis_codes[:, words], basis_scales[:, words]))
+                for pair in range(M_TILES // 2):
+                    acc = acc_psum.tile([P, 2, UNIT], F32, name="acc")
+                    for i in range(2):
+                        outputs = slice((2 * pair + i) * P, (2 * pair + i + 1) * P)
+                        for s in range(PASSES):
+                            codes, scales = moving[s]
+                            nc.tensor.matmul_mx(
+                                out=acc[:, i, :],
+                                lhsT=w_codes[:, s, outputs].bitcast(FP8X4),
+                                lhsT_scale=w_scales[:, s, outputs],
+                                rhs=codes.bitcast(FP8X4),
+                                rhs_scale=scales,
+                                start=(s == 0),
+                                stop=(s == PASSES - 1),
+                            )
+                    acc_tiles[(n, pair)] = acc
+
+            def finish(n):
+                b, piece = divmod(n, UNITS_PER_BATCH)
+                columns = slice(piece * UNIT, (piece + 1) * UNIT)
+                out_sb = out_pool.tile([P, M_TILES, UNIT], F32, name="out_sb")
+                for m in range(M_TILES):
+                    pair, i = divmod(m, 2)
+                    nc.vector.scalar_tensor_tensor(
+                        out=out_sb[:, m, :],
+                        in0=acc_tiles[(n, pair)][:, i, :],
+                        scalar=bias[:, m : m + 1],
+                        in1=x_tiles[b][:, m, columns],
+                        op0=ALU.add,
+                        op1=ALU.add,
+                    )
+                nc.sync.dma_start(
+                    out=out[b, :, columns].rearrange("(m p) c -> p m c", p=P), in_=out_sb[:]
+                )
+                if piece == UNITS_PER_BATCH - 1 and b + X_TILES < BATCH:
+                    load_x(b + X_TILES)
+
+            for n in range(UNITS + 2):
+                if n + 1 < UNITS:
+                    square_centre_0(n + 1)
+                if n < UNITS:
+                    exponentials(n)
+                if 0 <= n - 1 < UNITS:
+                    quantise_basis(n - 1)
+                    matmuls(n - 1)
+                if 0 <= n - 2:
+                    finish(n - 2)
+                if n + 1 < UNITS:
+                    square_centre_1(n + 1)

@@ -28,10 +28,12 @@ UNITS = BATCH * TOKENS // UNIT
 UNITS_PER_BATCH = TOKENS // UNIT
 UNIT_H = HALVES * UNIT * 2
 WORDS = HIDDEN // 2
-LOADS_AHEAD = 6
-COPIES_AHEAD = 2
-WEIGHT_BANKS = 2 * PASSES
-WEIGHT_EVERY = UNITS // WEIGHT_BANKS
+BANKS_AHEAD = 2
+H_BANKS = BANKS_AHEAD + 1
+LOAD_W_EVERY = 6
+LOTS = 2 * PASSES
+FIRST_LOT = UNITS // 2
+LOT_EVERY = (UNITS - FIRST_LOT) // LOTS
 X_TILES = 3
 
 FLOPS = 2 * BATCH * TOKENS * OUTS * (HIDDEN * CENTRES + HIDDEN)
@@ -42,21 +44,20 @@ def tile_kan1_pb_t_kernel(tc, h_mix, x, fc2_spline_w, fc2_base_w, fc2_base_b, ou
     with ExitStack() as stack:
         stack.enter_context(tc.manual_schedule())
         keep = stack.enter_context(tc.tile_pool(name="keep", bufs=1))
-        h_raw_pool = stack.enter_context(tc.tile_pool(name="h_raw", bufs=LOADS_AHEAD))
+        h_raw_pool = stack.enter_context(tc.tile_pool(name="h_raw", bufs=UNITS))
         w_pool = stack.enter_context(tc.tile_pool(name="w", bufs=PASSES))
         silu_pool = stack.enter_context(tc.tile_pool(name="silu", bufs=3))
         x_pool = stack.enter_context(tc.tile_pool(name="x", bufs=X_TILES))
         sq_pool = stack.enter_context(tc.tile_pool(name="sq", bufs=2))
         basis_pool = stack.enter_context(tc.tile_pool(name="basis", bufs=2))
         out_pool = stack.enter_context(tc.tile_pool(name="out", bufs=4))
+        h_psum = stack.enter_context(tc.psum_pool(name="h_bank", bufs=H_BANKS))
 
         ident = keep.tile([P, P], F32)
         make_identity(nc, ident[:])
         one_half = keep.tile([P, 1], F32)
         nc.vector.memset(one_half[:], 0.5)
         bias = keep.tile([P, M_TILES], F32)
-        h_t = keep.tile([P, UNITS * UNIT_H], BF16)
-        h_t_words = h_t[:].bitcast(F32)
         silu_codes = keep.tile([P, UNITS * UNIT], U32, align_bytes=64)
         silu_scales = keep.tile([P, UNITS * UNIT], U8, align_bytes=64)
         w_codes = keep.tile([P, PASSES, OUTS], U32, align_bytes=64)
@@ -94,31 +95,44 @@ def tile_kan1_pb_t_kernel(tc, h_mix, x, fc2_spline_w, fc2_base_w, fc2_base_b, ou
             nc.sync.dma_start(out=x_sb[:], in_=x[b].rearrange("(m p) c -> p m c", p=P))
             x_tiles[b] = x_sb
 
-        for n in range(LOADS_AHEAD):
+        for n in range(UNITS):
             load_h(n)
-        for s in range(PASSES):
-            load_weights(s)
+            if n % LOAD_W_EVERY == 0 and 0 < n // LOAD_W_EVERY <= PASSES:
+                load_weights(n // LOAD_W_EVERY - 1)
         bias_rows = keep.tile([P, P], BF16)
         nc.vector.memset(bias_rows[:].bitcast(I32), 0)
         nc.sync.dma_start(out=bias_rows[0:M_TILES, :], in_=fc2_base_b.rearrange("(m p) -> m p", p=P))
+        for b in range(X_TILES):
+            load_x(b)
+
+        h_banks = {}
+
+        def transpose_h(phase, n):
+            h_words = h_raw_tiles[n][:].bitcast(F32)
+            h_bank = h_psum.tile([P, HALVES * UNIT], F32, name="h_bank")
+            for t in range(UNIT // P):
+                for u in range(HALVES):
+                    nc.tensor.transpose(
+                        h_bank[:, u * UNIT + t * P : u * UNIT + (t + 1) * P],
+                        h_words[:, t * WORDS + u * P : t * WORDS + (u + 1) * P],
+                        ident[:],
+                    )
+            h_banks[(phase, n)] = h_bank[:].bitcast(BF16)
 
         sq_tiles = {}
         basis_bf_tiles = {}
         basis_mx_tiles = {}
 
-        def h_of_unit(n):
-            return h_t[:, n * UNIT_H : (n + 1) * UNIT_H]
-
         def square_centre_0(n):
             sq = sq_pool.tile([P, CENTRES, UNIT_H], F32, name="sq")
             nc.scalar.activation(
-                out=sq[:, 0, :], in_=h_of_unit(n), func=ACT.Square, scale=0.5, bias=one_half[:]
+                out=sq[:, 0, :], in_=h_banks[(2, n)], func=ACT.Square, scale=0.5, bias=one_half[:]
             )
             sq_tiles[n] = sq
 
         def square_centre_1(n):
             sq = sq_tiles[n]
-            nc.vector.tensor_tensor(out=sq[:, 1, :], in0=sq[:, 0, :], in1=h_of_unit(n), op=ALU.subtract)
+            nc.vector.tensor_tensor(out=sq[:, 1, :], in0=sq[:, 0, :], in1=h_banks[(2, n)], op=ALU.subtract)
 
         def exponentials(n):
             basis_bf = basis_pool.tile([P, UNIT_H, CENTRES], BF16, name="basis_bf", align_bytes=64)
@@ -140,29 +154,15 @@ def tile_kan1_pb_t_kernel(tc, h_mix, x, fc2_spline_w, fc2_base_w, fc2_base_b, ou
             )
             basis_mx_tiles[n] = (basis_codes, basis_scales)
 
-        with tc.psum_pool(name="h_bank", bufs=4) as h_psum, tc.psum_pool(name="w_bank", bufs=2) as w_psum:
+        with tc.psum_pool(name="w_bank", bufs=2) as w_psum:
             silu_bf_tiles = {}
             w_bf_tiles = {}
-
-            def transpose_h(n):
-                h_words = h_raw_tiles[n][:].bitcast(F32)
-                h_bank = h_psum.tile([P, HALVES * UNIT], F32, name="h_bank")
-                for t in range(UNIT // P):
-                    for u in range(HALVES):
-                        nc.tensor.transpose(
-                            h_bank[:, u * UNIT + t * P : u * UNIT + (t + 1) * P],
-                            h_words[:, t * WORDS + u * P : t * WORDS + (u + 1) * P],
-                            ident[:],
-                        )
-                nc.vector.tensor_copy(
-                    out=h_t_words[:, n * HALVES * UNIT : (n + 1) * HALVES * UNIT], in_=h_bank[:]
-                )
 
             def silu(n):
                 silu_bf = silu_pool.tile([P, UNIT_H], BF16, name="silu_bf", align_bytes=64)
                 nc.scalar.activation(
                     out=silu_bf[:].rearrange("p (w u e) -> p w u e", u=HALVES, e=2),
-                    in_=h_of_unit(n).rearrange("p (u w e) -> p w u e", u=HALVES, e=2),
+                    in_=h_banks[(1, n)].rearrange("p (u w e) -> p w u e", u=HALVES, e=2),
                     func=ACT.Silu,
                 )
                 silu_bf_tiles[n] = silu_bf
@@ -212,20 +212,18 @@ def tile_kan1_pb_t_kernel(tc, h_mix, x, fc2_spline_w, fc2_base_w, fc2_base_b, ou
                 nc.tensor.transpose(bias_bank[:], bias_rows_f32[:], ident[:])
                 nc.vector.tensor_copy(out=bias[:], in_=bias_bank[:, 0:M_TILES])
 
-            for n in range(COPIES_AHEAD):
-                transpose_h(n)
+            for n in range(BANKS_AHEAD):
+                transpose_h(1, n)
             for n in range(UNITS):
-                if n + LOADS_AHEAD < UNITS:
-                    load_h(n + LOADS_AHEAD)
-                if n + COPIES_AHEAD < UNITS:
-                    transpose_h(n + COPIES_AHEAD)
+                if n + BANKS_AHEAD < UNITS:
+                    transpose_h(1, n + BANKS_AHEAD)
+                else:
+                    transpose_h(2, n + BANKS_AHEAD - UNITS)
                 silu(n)
                 if n > 0:
                     quantise_silu(n - 1)
-                if n % WEIGHT_EVERY == WEIGHT_EVERY - 1:
-                    transpose_weights(n // WEIGHT_EVERY)
-            for b in range(X_TILES):
-                load_x(b)
+                if n >= FIRST_LOT and (n - FIRST_LOT) % LOT_EVERY == 0:
+                    transpose_weights((n - FIRST_LOT) // LOT_EVERY)
             square_centre_0(0)
             square_centre_1(0)
             quantise_silu(UNITS - 1)
@@ -233,7 +231,7 @@ def tile_kan1_pb_t_kernel(tc, h_mix, x, fc2_spline_w, fc2_base_w, fc2_base_b, ou
                 quantise_weights(s)
             transpose_bias()
 
-        with tc.psum_pool(name="acc", bufs=8) as acc_psum:
+        with tc.psum_pool(name="acc", bufs=4) as acc_psum:
             acc_tiles = {}
 
             def matmuls(n):
@@ -281,6 +279,8 @@ def tile_kan1_pb_t_kernel(tc, h_mix, x, fc2_spline_w, fc2_base_w, fc2_base_b, ou
                     load_x(b + X_TILES)
 
             for n in range(UNITS + 2):
+                if n + BANKS_AHEAD < UNITS:
+                    transpose_h(2, n + BANKS_AHEAD)
                 if n + 1 < UNITS:
                     square_centre_0(n + 1)
                 if n < UNITS:

@@ -35,6 +35,9 @@ LOTS = 2 * PASSES
 FIRST_LOT = UNITS // 2
 LOT_EVERY = (UNITS - FIRST_LOT) // LOTS
 X_TILES = 3
+VECTOR_EVERY = 4
+VECTOR_AHEAD = 4
+VECTOR_STEP = 4
 
 FLOPS = 2 * BATCH * TOKENS * OUTS * (HIDDEN * CENTRES + HIDDEN)
 
@@ -46,17 +49,22 @@ def tile_kan1_pb_t_kernel(tc, h_mix, x, fc2_spline_w, fc2_base_w, fc2_base_b, ou
         keep = stack.enter_context(tc.tile_pool(name="keep", bufs=1))
         h_raw_pool = stack.enter_context(tc.tile_pool(name="h_raw", bufs=UNITS))
         w_pool = stack.enter_context(tc.tile_pool(name="w", bufs=PASSES))
-        silu_pool = stack.enter_context(tc.tile_pool(name="silu", bufs=3))
+        silu_pool = stack.enter_context(tc.tile_pool(name="silu", bufs=6))
         x_pool = stack.enter_context(tc.tile_pool(name="x", bufs=X_TILES))
         sq_pool = stack.enter_context(tc.tile_pool(name="sq", bufs=2))
+        vector_sq_pool = stack.enter_context(tc.tile_pool(name="vector_sq", bufs=VECTOR_AHEAD))
+        h_sb_pool = stack.enter_context(tc.tile_pool(name="h_sb", bufs=2))
         basis_pool = stack.enter_context(tc.tile_pool(name="basis", bufs=2))
         out_pool = stack.enter_context(tc.tile_pool(name="out", bufs=4))
         h_psum = stack.enter_context(tc.psum_pool(name="h_bank", bufs=H_BANKS))
+        vector_psum = stack.enter_context(tc.psum_pool(name="vector_bank", bufs=1))
 
         ident = keep.tile([P, P], F32)
         make_identity(nc, ident[:])
-        one_half = keep.tile([P, 1], F32)
-        nc.vector.memset(one_half[:], 0.5)
+        one = keep.tile([P, 1], F32)
+        nc.vector.memset(one[:], 1.0)
+        minus_quarter = keep.tile([P, 1], F32)
+        nc.vector.memset(minus_quarter[:], -0.25)
         bias = keep.tile([P, M_TILES], F32)
         silu_codes = keep.tile([P, UNITS * UNIT], U32, align_bytes=64)
         silu_scales = keep.tile([P, UNITS * UNIT], U8, align_bytes=64)
@@ -107,9 +115,9 @@ def tile_kan1_pb_t_kernel(tc, h_mix, x, fc2_spline_w, fc2_base_w, fc2_base_b, ou
 
         h_banks = {}
 
-        def transpose_h(phase, n):
+        def transpose_h(phase, n, psum=h_psum):
             h_words = h_raw_tiles[n][:].bitcast(F32)
-            h_bank = h_psum.tile([P, HALVES * UNIT], F32, name="h_bank")
+            h_bank = psum.tile([P, HALVES * UNIT], F32, name="h_bank")
             for t in range(UNIT // P):
                 for u in range(HALVES):
                     nc.tensor.transpose(
@@ -118,30 +126,59 @@ def tile_kan1_pb_t_kernel(tc, h_mix, x, fc2_spline_w, fc2_base_w, fc2_base_b, ou
                         ident[:],
                     )
             h_banks[(phase, n)] = h_bank[:].bitcast(BF16)
+            return h_bank
 
         sq_tiles = {}
         basis_bf_tiles = {}
         basis_mx_tiles = {}
 
+        def is_vectors(n):
+            return n % VECTOR_EVERY == 0
+
         def square_centre_0(n):
             sq = sq_pool.tile([P, CENTRES, UNIT_H], F32, name="sq")
-            nc.scalar.activation(
-                out=sq[:, 0, :], in_=h_banks[(2, n)], func=ACT.Square, scale=0.5, bias=one_half[:]
-            )
+            nc.scalar.activation(out=sq[:, 0, :], in_=h_banks[(2, n)], func=ACT.Square, bias=one[:])
             sq_tiles[n] = sq
 
         def square_centre_1(n):
             sq = sq_tiles[n]
-            nc.vector.tensor_tensor(out=sq[:, 1, :], in0=sq[:, 0, :], in1=h_banks[(2, n)], op=ALU.subtract)
+            nc.vector.scalar_tensor_tensor(
+                out=sq[:, 1, :], in0=h_banks[(2, n)], scalar=-4.0, in1=sq[:, 0, :], op0=ALU.mult, op1=ALU.add
+            )
+
+        def vector_squares(n):
+            h_bank = transpose_h(2, n, psum=vector_psum)
+            h_sb = h_sb_pool.tile([P, HALVES * UNIT], F32, name="h_sb")
+            nc.vector.tensor_copy(out=h_sb[:], in_=h_bank[:])
+            sq = vector_sq_pool.tile([P, CENTRES, UNIT_H], F32, name="vector_sq")
+            for i in range(CENTRES):
+                nc.vector.scalar_tensor_tensor(
+                    out=sq[:, i, :],
+                    in0=h_banks[(2, n)],
+                    scalar=2.0 - 4.0 * i,
+                    in1=h_sb[:].bitcast(BF16),
+                    op0=ALU.add,
+                    op1=ALU.mult,
+                )
+            sq_tiles[n] = sq
 
         def exponentials(n):
             basis_bf = basis_pool.tile([P, UNIT_H, CENTRES], BF16, name="basis_bf", align_bytes=64)
-            nc.scalar.activation(
-                out=basis_bf[:],
-                in_=sq_tiles[n][:].rearrange("p i c -> p c i"),
-                func=ACT.Exp,
-                scale=-1.0,
-            )
+            if is_vectors(n):
+                nc.scalar.activation(
+                    out=basis_bf[:],
+                    in_=sq_tiles[n][:].rearrange("p i c -> p c i"),
+                    func=ACT.Exp,
+                    scale=-0.25,
+                    bias=minus_quarter[:],
+                )
+            else:
+                nc.scalar.activation(
+                    out=basis_bf[:],
+                    in_=sq_tiles[n][:].rearrange("p i c -> p c i"),
+                    func=ACT.Exp,
+                    scale=-0.25,
+                )
             basis_bf_tiles[n] = basis_bf
 
         def quantise_basis(n):
@@ -217,15 +254,15 @@ def tile_kan1_pb_t_kernel(tc, h_mix, x, fc2_spline_w, fc2_base_w, fc2_base_b, ou
             for n in range(UNITS):
                 if n + BANKS_AHEAD < UNITS:
                     transpose_h(1, n + BANKS_AHEAD)
-                else:
+                elif not is_vectors(n + BANKS_AHEAD - UNITS):
                     transpose_h(2, n + BANKS_AHEAD - UNITS)
                 silu(n)
                 if n > 0:
                     quantise_silu(n - 1)
+                if n % VECTOR_STEP == 1 and n // VECTOR_STEP < VECTOR_AHEAD:
+                    vector_squares(n // VECTOR_STEP * VECTOR_EVERY)
                 if n >= FIRST_LOT and (n - FIRST_LOT) % LOT_EVERY == 0:
                     transpose_weights((n - FIRST_LOT) // LOT_EVERY)
-            square_centre_0(0)
-            square_centre_1(0)
             quantise_silu(UNITS - 1)
             for s in range(PASSES):
                 quantise_weights(s)
@@ -279,9 +316,9 @@ def tile_kan1_pb_t_kernel(tc, h_mix, x, fc2_spline_w, fc2_base_w, fc2_base_b, ou
                     load_x(b + X_TILES)
 
             for n in range(UNITS + 2):
-                if n + BANKS_AHEAD < UNITS:
+                if n + BANKS_AHEAD < UNITS and not is_vectors(n + BANKS_AHEAD):
                     transpose_h(2, n + BANKS_AHEAD)
-                if n + 1 < UNITS:
+                if n + 1 < UNITS and not is_vectors(n + 1):
                     square_centre_0(n + 1)
                 if n < UNITS:
                     exponentials(n)
@@ -290,5 +327,7 @@ def tile_kan1_pb_t_kernel(tc, h_mix, x, fc2_spline_w, fc2_base_w, fc2_base_b, ou
                     matmuls(n - 1)
                 if 0 <= n - 2:
                     finish(n - 2)
-                if n + 1 < UNITS:
+                if n + 1 < UNITS and not is_vectors(n + 1):
                     square_centre_1(n + 1)
+                if is_vectors(n) and n + VECTOR_EVERY * VECTOR_AHEAD < UNITS:
+                    vector_squares(n + VECTOR_EVERY * VECTOR_AHEAD)

@@ -35,11 +35,20 @@ LOTS = 2 * PASSES
 FIRST_LOT = UNITS // 2
 LOT_EVERY = (UNITS - FIRST_LOT) // LOTS
 X_TILES = 3
+SQUARES_AHEAD = 2
 VECTOR_EVERY = 4
 VECTOR_AHEAD = 4
 VECTOR_STEP = 4
 
 FLOPS = 2 * BATCH * TOKENS * OUTS * (HIDDEN * CENTRES + HIDDEN)
+
+
+def is_vectors(n):
+    return 0 <= n < UNITS and n % VECTOR_EVERY == 0
+
+
+def is_scalars(n):
+    return 0 <= n < UNITS and n % VECTOR_EVERY != 0
 
 
 def tile_kan1_pb_t_kernel(tc, h_mix, x, fc2_spline_w, fc2_base_w, fc2_base_b, out):
@@ -48,14 +57,11 @@ def tile_kan1_pb_t_kernel(tc, h_mix, x, fc2_spline_w, fc2_base_w, fc2_base_b, ou
         stack.enter_context(tc.manual_schedule())
         keep = stack.enter_context(tc.tile_pool(name="keep", bufs=1))
         h_raw_pool = stack.enter_context(tc.tile_pool(name="h_raw", bufs=UNITS))
-        w_pool = stack.enter_context(tc.tile_pool(name="w", bufs=PASSES))
         silu_pool = stack.enter_context(tc.tile_pool(name="silu", bufs=6))
         x_pool = stack.enter_context(tc.tile_pool(name="x", bufs=X_TILES))
-        sq_pool = stack.enter_context(tc.tile_pool(name="sq", bufs=2))
+        sq_pool = stack.enter_context(tc.tile_pool(name="sq", bufs=SQUARES_AHEAD + 1))
         vector_sq_pool = stack.enter_context(tc.tile_pool(name="vector_sq", bufs=VECTOR_AHEAD))
         h_sb_pool = stack.enter_context(tc.tile_pool(name="h_sb", bufs=2))
-        basis_pool = stack.enter_context(tc.tile_pool(name="basis", bufs=2))
-        out_pool = stack.enter_context(tc.tile_pool(name="out", bufs=4))
         h_psum = stack.enter_context(tc.psum_pool(name="h_bank", bufs=H_BANKS))
         vector_psum = stack.enter_context(tc.psum_pool(name="vector_bank", bufs=1))
 
@@ -73,6 +79,8 @@ def tile_kan1_pb_t_kernel(tc, h_mix, x, fc2_spline_w, fc2_base_w, fc2_base_b, ou
 
         h_rows = h_mix.rearrange("b c j -> (b c) j")
         h_raw_tiles = {}
+        h_banks = {}
+        x_tiles = {}
 
         def load_h(n):
             h_raw = h_raw_pool.tile([P, (UNIT // P) * HIDDEN], BF16, name="h_raw")
@@ -82,38 +90,10 @@ def tile_kan1_pb_t_kernel(tc, h_mix, x, fc2_spline_w, fc2_base_w, fc2_base_b, ou
             )
             h_raw_tiles[n] = h_raw
 
-        w_raw_tiles = {}
-
-        def load_weights(s):
-            w_raw = w_pool.tile([P, M_TILES * K_PASS], BF16, name="w_raw")
-            if s == 0:
-                columns = fc2_base_w
-            else:
-                columns = fc2_spline_w[:, (s - 1) * K_PASS : s * K_PASS]
-            nc.sync.dma_start(
-                out=w_raw[:].rearrange("r (m k) -> r m k", k=K_PASS),
-                in_=columns.rearrange("(m r) k -> r m k", r=P),
-            )
-            w_raw_tiles[s] = w_raw
-
-        x_tiles = {}
-
         def load_x(b):
             x_sb = x_pool.tile([P, M_TILES, TOKENS], BF16, name="x_sb")
             nc.sync.dma_start(out=x_sb[:], in_=x[b].rearrange("(m p) c -> p m c", p=P))
             x_tiles[b] = x_sb
-
-        for n in range(UNITS):
-            load_h(n)
-            if n % LOAD_W_EVERY == 0 and 0 < n // LOAD_W_EVERY <= PASSES:
-                load_weights(n // LOAD_W_EVERY - 1)
-        bias_rows = keep.tile([P, P], BF16)
-        nc.vector.memset(bias_rows[:].bitcast(I32), 0)
-        nc.sync.dma_start(out=bias_rows[0:M_TILES, :], in_=fc2_base_b.rearrange("(m p) -> m p", p=P))
-        for b in range(X_TILES):
-            load_x(b)
-
-        h_banks = {}
 
         def transpose_h(phase, n, psum=h_psum):
             h_words = h_raw_tiles[n][:].bitcast(F32)
@@ -129,11 +109,6 @@ def tile_kan1_pb_t_kernel(tc, h_mix, x, fc2_spline_w, fc2_base_w, fc2_base_b, ou
             return h_bank
 
         sq_tiles = {}
-        basis_bf_tiles = {}
-        basis_mx_tiles = {}
-
-        def is_vectors(n):
-            return n % VECTOR_EVERY == 0
 
         def square_centre_0(n):
             sq = sq_pool.tile([P, CENTRES, UNIT_H], F32, name="sq")
@@ -162,38 +137,22 @@ def tile_kan1_pb_t_kernel(tc, h_mix, x, fc2_spline_w, fc2_base_w, fc2_base_b, ou
                 )
             sq_tiles[n] = sq
 
-        def exponentials(n):
-            basis_bf = basis_pool.tile([P, UNIT_H, CENTRES], BF16, name="basis_bf", align_bytes=64)
-            if is_vectors(n):
-                nc.scalar.activation(
-                    out=basis_bf[:],
-                    in_=sq_tiles[n][:].rearrange("p i c -> p c i"),
-                    func=ACT.Exp,
-                    scale=-0.25,
-                    bias=minus_quarter[:],
-                )
-            else:
-                nc.scalar.activation(
-                    out=basis_bf[:],
-                    in_=sq_tiles[n][:].rearrange("p i c -> p c i"),
-                    func=ACT.Exp,
-                    scale=-0.25,
-                )
-            basis_bf_tiles[n] = basis_bf
-
-        def quantise_basis(n):
-            basis_codes = basis_pool.tile([P, HALVES * UNIT], U32, name="basis_codes", align_bytes=64)
-            basis_scales = basis_pool.tile([P, HALVES * UNIT], U8, name="basis_scales", align_bytes=64)
-            nc.vector.quantize_mx(
-                out=basis_codes[:].bitcast(FP8X4),
-                scales=basis_scales[:],
-                in_=basis_bf_tiles[n][:].rearrange("p c i -> p (c i)"),
-            )
-            basis_mx_tiles[n] = (basis_codes, basis_scales)
-
-        with tc.psum_pool(name="w_bank", bufs=2) as w_psum:
-            silu_bf_tiles = {}
+        with tc.tile_pool(name="w", bufs=PASSES) as w_pool, tc.psum_pool(name="w_bank", bufs=2) as w_psum:
+            w_raw_tiles = {}
             w_bf_tiles = {}
+            silu_bf_tiles = {}
+
+            def load_weights(s):
+                w_raw = w_pool.tile([P, M_TILES * K_PASS], BF16, name="w_raw")
+                if s == 0:
+                    columns = fc2_base_w
+                else:
+                    columns = fc2_spline_w[:, (s - 1) * K_PASS : s * K_PASS]
+                nc.sync.dma_start(
+                    out=w_raw[:].rearrange("r (m k) -> r m k", k=K_PASS),
+                    in_=columns.rearrange("(m r) k -> r m k", r=P),
+                )
+                w_raw_tiles[s] = w_raw
 
             def silu(n):
                 silu_bf = silu_pool.tile([P, UNIT_H], BF16, name="silu_bf", align_bytes=64)
@@ -249,27 +208,73 @@ def tile_kan1_pb_t_kernel(tc, h_mix, x, fc2_spline_w, fc2_base_w, fc2_base_b, ou
                 nc.tensor.transpose(bias_bank[:], bias_rows_f32[:], ident[:])
                 nc.vector.tensor_copy(out=bias[:], in_=bias_bank[:, 0:M_TILES])
 
+            bias_rows = keep.tile([P, P], BF16)
+            nc.vector.memset(bias_rows[:].bitcast(I32), 0)
+            for n in range(UNITS):
+                load_h(n)
+                if n == BANKS_AHEAD - 1:
+                    nc.sync.dma_start(
+                        out=bias_rows[0:M_TILES, :], in_=fc2_base_b.rearrange("(m p) -> m p", p=P)
+                    )
+                if n % LOAD_W_EVERY == 0 and 0 < n // LOAD_W_EVERY <= PASSES:
+                    load_weights(n // LOAD_W_EVERY - 1)
+            for b in range(X_TILES):
+                load_x(b)
+
             for n in range(BANKS_AHEAD):
                 transpose_h(1, n)
+            transpose_bias()
             for n in range(UNITS):
                 if n + BANKS_AHEAD < UNITS:
                     transpose_h(1, n + BANKS_AHEAD)
-                elif not is_vectors(n + BANKS_AHEAD - UNITS):
-                    transpose_h(2, n + BANKS_AHEAD - UNITS)
                 silu(n)
                 if n > 0:
                     quantise_silu(n - 1)
                 if n % VECTOR_STEP == 1 and n // VECTOR_STEP < VECTOR_AHEAD:
                     vector_squares(n // VECTOR_STEP * VECTOR_EVERY)
                 if n >= FIRST_LOT and (n - FIRST_LOT) % LOT_EVERY == 0:
-                    transpose_weights((n - FIRST_LOT) // LOT_EVERY)
+                    s, pair = divmod((n - FIRST_LOT) // LOT_EVERY, 2)
+                    if pair == 0 and s > 0:
+                        quantise_weights(s - 1)
+                    transpose_weights(2 * s + pair)
             quantise_silu(UNITS - 1)
-            for s in range(PASSES):
-                quantise_weights(s)
-            transpose_bias()
+            quantise_weights(PASSES - 1)
 
-        with tc.psum_pool(name="acc", bufs=4) as acc_psum:
+        with tc.tile_pool(name="basis", bufs=2) as basis_pool, tc.tile_pool(
+            name="out", bufs=4
+        ) as out_pool, tc.psum_pool(name="acc", bufs=4) as acc_psum:
+            basis_bf_tiles = {}
+            basis_mx_tiles = {}
             acc_tiles = {}
+
+            def exponentials(n):
+                basis_bf = basis_pool.tile([P, UNIT_H, CENTRES], BF16, name="basis_bf", align_bytes=64)
+                if is_vectors(n):
+                    nc.scalar.activation(
+                        out=basis_bf[:],
+                        in_=sq_tiles[n][:].rearrange("p i c -> p c i"),
+                        func=ACT.Exp,
+                        scale=-0.25,
+                        bias=minus_quarter[:],
+                    )
+                else:
+                    nc.scalar.activation(
+                        out=basis_bf[:],
+                        in_=sq_tiles[n][:].rearrange("p i c -> p c i"),
+                        func=ACT.Exp,
+                        scale=-0.25,
+                    )
+                basis_bf_tiles[n] = basis_bf
+
+            def quantise_basis(n):
+                basis_codes = basis_pool.tile([P, HALVES * UNIT], U32, name="basis_codes", align_bytes=64)
+                basis_scales = basis_pool.tile([P, HALVES * UNIT], U8, name="basis_scales", align_bytes=64)
+                nc.vector.quantize_mx(
+                    out=basis_codes[:].bitcast(FP8X4),
+                    scales=basis_scales[:],
+                    in_=basis_bf_tiles[n][:].rearrange("p c i -> p (c i)"),
+                )
+                basis_mx_tiles[n] = (basis_codes, basis_scales)
 
             def matmuls(n):
                 basis_codes, basis_scales = basis_mx_tiles[n]
@@ -315,19 +320,19 @@ def tile_kan1_pb_t_kernel(tc, h_mix, x, fc2_spline_w, fc2_base_w, fc2_base_b, ou
                 if piece == UNITS_PER_BATCH - 1 and b + X_TILES < BATCH:
                     load_x(b + X_TILES)
 
-            for n in range(UNITS + 2):
-                if n + BANKS_AHEAD < UNITS and not is_vectors(n + BANKS_AHEAD):
-                    transpose_h(2, n + BANKS_AHEAD)
-                if n + 1 < UNITS and not is_vectors(n + 1):
-                    square_centre_0(n + 1)
-                if n < UNITS:
+            for n in range(-SQUARES_AHEAD - 1, UNITS + 2):
+                if is_scalars(n + SQUARES_AHEAD + 1):
+                    transpose_h(2, n + SQUARES_AHEAD + 1)
+                if is_scalars(n + SQUARES_AHEAD):
+                    square_centre_0(n + SQUARES_AHEAD)
+                if 0 <= n < UNITS:
                     exponentials(n)
                 if 0 <= n - 1 < UNITS:
                     quantise_basis(n - 1)
                     matmuls(n - 1)
-                if 0 <= n - 2:
+                if 0 <= n - 2 < UNITS:
                     finish(n - 2)
-                if n + 1 < UNITS and not is_vectors(n + 1):
-                    square_centre_1(n + 1)
-                if is_vectors(n) and n + VECTOR_EVERY * VECTOR_AHEAD < UNITS:
+                if is_scalars(n + SQUARES_AHEAD):
+                    square_centre_1(n + SQUARES_AHEAD)
+                if is_vectors(n) and is_vectors(n + VECTOR_EVERY * VECTOR_AHEAD):
                     vector_squares(n + VECTOR_EVERY * VECTOR_AHEAD)

@@ -35,7 +35,7 @@ LOTS = 2 * PASSES
 FIRST_LOT = UNITS // 2
 LOT_EVERY = (UNITS - FIRST_LOT) // LOTS
 X_TILES = 3
-SQUARES_AHEAD = 2
+SQUARES_AHEAD = 3
 VECTOR_EVERY = 4
 VECTOR_AHEAD = 4
 VECTOR_STEP = 4
@@ -240,8 +240,8 @@ def tile_kan1_pb_t_kernel(tc, h_mix, x, fc2_spline_w, fc2_base_w, fc2_base_b, ou
             quantise_silu(UNITS - 1)
             quantise_weights(PASSES - 1)
 
-        with tc.tile_pool(name="basis", bufs=2) as basis_pool, tc.tile_pool(
-            name="out", bufs=4
+        with tc.tile_pool(name="basis", bufs=3) as basis_pool, tc.tile_pool(
+            name="out", bufs=8
         ) as out_pool, tc.psum_pool(name="acc", bufs=4) as acc_psum:
             basis_bf_tiles = {}
             basis_mx_tiles = {}
@@ -303,20 +303,22 @@ def tile_kan1_pb_t_kernel(tc, h_mix, x, fc2_spline_w, fc2_base_w, fc2_base_b, ou
             def finish(n):
                 b, piece = divmod(n, UNITS_PER_BATCH)
                 columns = slice(piece * UNIT, (piece + 1) * UNIT)
-                out_sb = out_pool.tile([P, M_TILES, UNIT], F32, name="out_sb")
-                for m in range(M_TILES):
-                    pair, i = divmod(m, 2)
-                    nc.vector.scalar_tensor_tensor(
-                        out=out_sb[:, m, :],
-                        in0=acc_tiles[(n, pair)][:, i, :],
-                        scalar=bias[:, m : m + 1],
-                        in1=x_tiles[b][:, m, columns],
-                        op0=ALU.add,
-                        op1=ALU.add,
+                for pair in range(M_TILES // 2):
+                    out_sb = out_pool.tile([P, 2, UNIT], F32, name="out_sb")
+                    for i in range(2):
+                        m = 2 * pair + i
+                        nc.vector.scalar_tensor_tensor(
+                            out=out_sb[:, i, :],
+                            in0=acc_tiles[(n, pair)][:, i, :],
+                            scalar=bias[:, m : m + 1],
+                            in1=x_tiles[b][:, m, columns],
+                            op0=ALU.add,
+                            op1=ALU.add,
+                        )
+                    rows = slice(2 * pair * P, 2 * (pair + 1) * P)
+                    nc.sync.dma_start(
+                        out=out[b, rows, columns].rearrange("(i p) c -> p i c", p=P), in_=out_sb[:]
                     )
-                nc.sync.dma_start(
-                    out=out[b, :, columns].rearrange("(m p) c -> p m c", p=P), in_=out_sb[:]
-                )
                 if piece == UNITS_PER_BATCH - 1 and b + X_TILES < BATCH:
                     load_x(b + X_TILES)
 

@@ -29,7 +29,18 @@ UNITS_PER_BATCH = TOKENS // UNIT
 UNIT_H = HALVES * UNIT * 2
 WORDS = HIDDEN // 2
 BANKS_AHEAD = 2
-H_BANKS = BANKS_AHEAD + 1
+H_BANKS = 4
+VECTOR_BANKS = 1
+ACC_BANKS = 3
+TENSOR_EVERY = 4
+TENSOR_FIRST = 1
+TENSOR_TILES = 3
+TENSOR_JOB = 4
+SPLIT_FILL = 1
+BASIS_TILES = 3
+OUT_TILES = 8
+SQ_TILES = 4
+TENSOR_EARLY = 3
 LOAD_W_EVERY = 6
 LOTS = 2 * PASSES
 FIRST_LOT = UNITS // 2
@@ -38,6 +49,7 @@ X_TILES = 3
 SQUARES_AHEAD = 3
 VECTOR_EVERY = 4
 VECTOR_AHEAD = 4
+VECTOR_FIRST = 3
 VECTOR_STEP = 4
 
 FLOPS = 2 * BATCH * TOKENS * OUTS * (HIDDEN * CENTRES + HIDDEN)
@@ -47,8 +59,12 @@ def is_vectors(n):
     return 0 <= n < UNITS and n % VECTOR_EVERY == 0
 
 
+def is_tensors(n):
+    return 0 <= n < UNITS and n % TENSOR_EVERY == TENSOR_FIRST and not is_vectors(n)
+
+
 def is_scalars(n):
-    return 0 <= n < UNITS and n % VECTOR_EVERY != 0
+    return 0 <= n < UNITS and not is_vectors(n) and not is_tensors(n)
 
 
 def tile_kan1_pb_t_kernel(tc, h_mix, x, fc2_spline_w, fc2_base_w, fc2_base_b, out):
@@ -57,16 +73,20 @@ def tile_kan1_pb_t_kernel(tc, h_mix, x, fc2_spline_w, fc2_base_w, fc2_base_b, ou
         stack.enter_context(tc.manual_schedule())
         keep = stack.enter_context(tc.tile_pool(name="keep", bufs=1))
         h_raw_pool = stack.enter_context(tc.tile_pool(name="h_raw", bufs=UNITS))
-        silu_pool = stack.enter_context(tc.tile_pool(name="silu", bufs=6))
+        tensor_sq_pool = stack.enter_context(tc.tile_pool(name="tensor_sq", bufs=TENSOR_TILES))
         x_pool = stack.enter_context(tc.tile_pool(name="x", bufs=X_TILES))
-        sq_pool = stack.enter_context(tc.tile_pool(name="sq", bufs=SQUARES_AHEAD + 1))
+        sq_pool = stack.enter_context(tc.tile_pool(name="sq", bufs=SQ_TILES))
         vector_sq_pool = stack.enter_context(tc.tile_pool(name="vector_sq", bufs=VECTOR_AHEAD))
         h_sb_pool = stack.enter_context(tc.tile_pool(name="h_sb", bufs=2))
         h_psum = stack.enter_context(tc.psum_pool(name="h_bank", bufs=H_BANKS))
-        vector_psum = stack.enter_context(tc.psum_pool(name="vector_bank", bufs=1))
+        vector_psum = stack.enter_context(tc.psum_pool(name="vector_bank", bufs=VECTOR_BANKS))
 
         ident = keep.tile([P, P], F32)
         make_identity(nc, ident[:])
+        minus_four = keep.tile([P, P], BF16)
+        nc.vector.tensor_scalar(
+            out=minus_four[:], in0=ident[:], scalar1=-4.0, scalar2=0.0, op0=ALU.mult, op1=ALU.add
+        )
         one = keep.tile([P, 1], F32)
         nc.vector.memset(one[:], 1.0)
         minus_quarter = keep.tile([P, 1], F32)
@@ -137,7 +157,47 @@ def tile_kan1_pb_t_kernel(tc, h_mix, x, fc2_spline_w, fc2_base_w, fc2_base_b, ou
                 )
             sq_tiles[n] = sq
 
-        with tc.tile_pool(name="w", bufs=PASSES) as w_pool, tc.psum_pool(name="w_bank", bufs=2) as w_psum:
+        def tensor_square_0(n):
+            sq = tensor_sq_pool.tile([P, 2, UNIT // P * WORDS], F32, name="tensor_sq")
+            h = h_raw_tiles[n][:].rearrange("r (q e) -> r e q", e=2)
+            nc.vector.scalar_tensor_tensor(
+                out=sq[:], in0=h, scalar=2.0, in1=h, op0=ALU.add, op1=ALU.mult
+            )
+            sq_tiles[n] = sq
+
+        tensor_banks = {}
+
+        def tensor_squares(n, t):
+            banks = []
+            for u in range(HALVES):
+                bank = h_psum.tile([P, 2, CENTRES, P], F32, name="h_bank")
+                banks.append(bank)
+                tensor_banks[(n, t, u)] = bank
+
+            def z_0(u, e):
+                return sq_tiles[n][:, e, t * WORDS + u * P : t * WORDS + (u + 1) * P]
+
+            for e in range(2):
+                for u in range(HALVES):
+                    if e == 0:
+                        for both in range(2):
+                            nc.tensor.transpose(banks[u][:, both, 0, :], z_0(u, both), ident[:])
+                    nc.tensor.matmul(
+                        out=banks[u][:, e, 1, :], lhsT=z_0(u, e), rhs=ident[:], start=True, stop=False, is_transpose=True
+                    )
+                for u in range(HALVES):
+                    first = t * HIDDEN + u * 2 * P + e
+                    nc.tensor.matmul(
+                        out=banks[u][:, e, 1, :],
+                        lhsT=h_raw_tiles[n][:, first : first + 2 * P - 1 : 2],
+                        rhs=minus_four[:],
+                        start=False,
+                        stop=True,
+                    )
+
+        with tc.tile_pool(name="w", bufs=PASSES) as w_pool, tc.tile_pool(
+            name="silu", bufs=6
+        ) as silu_pool, tc.psum_pool(name="w_bank", bufs=2) as w_psum:
             w_raw_tiles = {}
             w_bf_tiles = {}
             silu_bf_tiles = {}
@@ -230,7 +290,9 @@ def tile_kan1_pb_t_kernel(tc, h_mix, x, fc2_spline_w, fc2_base_w, fc2_base_b, ou
                 silu(n)
                 if n > 0:
                     quantise_silu(n - 1)
-                if n % VECTOR_STEP == 1 and n // VECTOR_STEP < VECTOR_AHEAD:
+                if is_tensors(n) and n // TENSOR_EVERY < TENSOR_EARLY:
+                    tensor_square_0(n)
+                if n % VECTOR_STEP == VECTOR_FIRST and n // VECTOR_STEP < VECTOR_AHEAD:
                     vector_squares(n // VECTOR_STEP * VECTOR_EVERY)
                 if n >= FIRST_LOT and (n - FIRST_LOT) % LOT_EVERY == 0:
                     s, pair = divmod((n - FIRST_LOT) // LOT_EVERY, 2)
@@ -240,16 +302,27 @@ def tile_kan1_pb_t_kernel(tc, h_mix, x, fc2_spline_w, fc2_base_w, fc2_base_b, ou
             quantise_silu(UNITS - 1)
             quantise_weights(PASSES - 1)
 
-        with tc.tile_pool(name="basis", bufs=3) as basis_pool, tc.tile_pool(
-            name="out", bufs=8
-        ) as out_pool, tc.psum_pool(name="acc", bufs=4) as acc_psum:
+        with tc.tile_pool(name="basis", bufs=BASIS_TILES) as basis_pool, tc.tile_pool(
+            name="out", bufs=OUT_TILES
+        ) as out_pool, tc.psum_pool(name="acc", bufs=ACC_BANKS) as acc_psum:
             basis_bf_tiles = {}
             basis_mx_tiles = {}
             acc_tiles = {}
 
             def exponentials(n):
                 basis_bf = basis_pool.tile([P, UNIT_H, CENTRES], BF16, name="basis_bf", align_bytes=64)
-                if is_vectors(n):
+                if is_tensors(n):
+                    for t in range(UNIT // P):
+                        for u in range(HALVES):
+                            first = (u * UNIT + t * P) * 2
+                            nc.scalar.activation(
+                                out=basis_bf[:, first : first + 2 * P, :].rearrange("p (w e) i -> p w (e i)", e=2),
+                                in_=tensor_banks[(n, t, u)][:].rearrange("p e i w -> p w (e i)"),
+                                func=ACT.Exp,
+                                scale=-0.25,
+                                bias=minus_quarter[:],
+                            )
+                elif is_vectors(n):
                     nc.scalar.activation(
                         out=basis_bf[:],
                         in_=sq_tiles[n][:].rearrange("p i c -> p c i"),
@@ -325,6 +398,12 @@ def tile_kan1_pb_t_kernel(tc, h_mix, x, fc2_spline_w, fc2_base_w, fc2_base_b, ou
             for n in range(-SQUARES_AHEAD - 1, UNITS + 2):
                 if is_scalars(n + SQUARES_AHEAD + 1):
                     transpose_h(2, n + SQUARES_AHEAD + 1)
+                if is_tensors(n) and SPLIT_FILL:
+                    tensor_squares(n, 1)
+                if is_tensors(n + 1):
+                    tensor_squares(n + 1, 0)
+                    if not SPLIT_FILL:
+                        tensor_squares(n + 1, 1)
                 if is_scalars(n + SQUARES_AHEAD):
                     square_centre_0(n + SQUARES_AHEAD)
                 if 0 <= n < UNITS:
@@ -336,5 +415,7 @@ def tile_kan1_pb_t_kernel(tc, h_mix, x, fc2_spline_w, fc2_base_w, fc2_base_b, ou
                     finish(n - 2)
                 if is_scalars(n + SQUARES_AHEAD):
                     square_centre_1(n + SQUARES_AHEAD)
+                if is_tensors(n + TENSOR_JOB) and (n + TENSOR_JOB) // TENSOR_EVERY >= TENSOR_EARLY:
+                    tensor_square_0(n + TENSOR_JOB)
                 if is_vectors(n) and is_vectors(n + VECTOR_EVERY * VECTOR_AHEAD):
                     vector_squares(n + VECTOR_EVERY * VECTOR_AHEAD)

@@ -70,7 +70,11 @@ def is_scalars(n):
 def tile_kan1_pb_t_kernel(tc, h_mix, x, fc2_spline_w, fc2_base_w, fc2_base_b, out):
     nc = tc.nc
     with ExitStack() as stack:
-        stack.enter_context(tc.manual_schedule())
+        stack.enter_context(
+            tc.manual_schedule(
+                engines={mybir.EngineType.Activation, mybir.EngineType.DVE, mybir.EngineType.Pool, mybir.EngineType.SP}
+            )
+        )
         keep = stack.enter_context(tc.tile_pool(name="keep", bufs=1))
         h_raw_pool = stack.enter_context(tc.tile_pool(name="h_raw", bufs=UNITS))
         tensor_sq_pool = stack.enter_context(tc.tile_pool(name="tensor_sq", bufs=TENSOR_TILES))

@@ -29,18 +29,31 @@ UNITS_PER_BATCH = TOKENS // UNIT
 UNIT_H = HALVES * UNIT * 2
 WORDS = HIDDEN // 2
 BANKS_AHEAD = 2
-H_BANKS = 4
+H_BANKS = 5
 VECTOR_BANKS = 1
 ACC_BANKS = 3
-TENSOR_EVERY = 4
-TENSOR_FIRST = 1
+TENSOR_EVERY = 6
+TENSOR_FIRST = 3
 TENSOR_TILES = 3
 TENSOR_JOB = 4
 SPLIT_FILL = 1
 BASIS_TILES = 3
 OUT_TILES = 8
-SQ_TILES = 4
-TENSOR_EARLY = 3
+SQ_TILES = 3
+ROUND = "BUAA"
+TENSOR_LATE = 4
+GROUP = 2
+MERGE = 1
+VECTOR_TILES = 5
+SILU_GROUP = 2
+SILU_TILES = 4
+TAIL = 0
+MM_LAG = 1
+FIN_LAG = 1
+FILL_0 = 1
+FILL_1 = 0
+ORDER = "qfsub"
+TR_AHEAD = 4
 LOAD_W_EVERY = 6
 LOTS = 2 * PASSES
 FIRST_LOT = UNITS // 2
@@ -49,22 +62,26 @@ X_TILES = 3
 SQUARES_AHEAD = 3
 VECTOR_EVERY = 4
 VECTOR_AHEAD = 4
-VECTOR_FIRST = 3
+VECTOR_FIRST = 1
 VECTOR_STEP = 4
 
 FLOPS = 2 * BATCH * TOKENS * OUTS * (HIDDEN * CENTRES + HIDDEN)
 
 
+def kind(n):
+    return ROUND[n % len(ROUND)] if 0 <= n < UNITS else "none"
+
+
 def is_vectors(n):
-    return 0 <= n < UNITS and n % VECTOR_EVERY == 0
+    return kind(n) == "B"
 
 
 def is_tensors(n):
-    return 0 <= n < UNITS and n % TENSOR_EVERY == TENSOR_FIRST and not is_vectors(n)
+    return kind(n) == "U"
 
 
 def is_scalars(n):
-    return 0 <= n < UNITS and not is_vectors(n) and not is_tensors(n)
+    return kind(n) == "A"
 
 
 def tile_kan1_pb_t_kernel(tc, h_mix, x, fc2_spline_w, fc2_base_w, fc2_base_b, out):
@@ -80,10 +97,10 @@ def tile_kan1_pb_t_kernel(tc, h_mix, x, fc2_spline_w, fc2_base_w, fc2_base_b, ou
         tensor_sq_pool = stack.enter_context(tc.tile_pool(name="tensor_sq", bufs=TENSOR_TILES))
         x_pool = stack.enter_context(tc.tile_pool(name="x", bufs=X_TILES))
         sq_pool = stack.enter_context(tc.tile_pool(name="sq", bufs=SQ_TILES))
-        vector_sq_pool = stack.enter_context(tc.tile_pool(name="vector_sq", bufs=VECTOR_AHEAD))
+        vector_sq_pool = stack.enter_context(tc.tile_pool(name="vector_sq", bufs=VECTOR_TILES))
         h_sb_pool = stack.enter_context(tc.tile_pool(name="h_sb", bufs=2))
         h_psum = stack.enter_context(tc.psum_pool(name="h_bank", bufs=H_BANKS))
-        vector_psum = stack.enter_context(tc.psum_pool(name="vector_bank", bufs=VECTOR_BANKS))
+        vector_psum = h_psum if MERGE else stack.enter_context(tc.psum_pool(name="vector_bank", bufs=VECTOR_BANKS))
 
         ident = keep.tile([P, P], F32)
         make_identity(nc, ident[:])
@@ -171,28 +188,27 @@ def tile_kan1_pb_t_kernel(tc, h_mix, x, fc2_spline_w, fc2_base_w, fc2_base_b, ou
 
         tensor_banks = {}
 
-        def tensor_squares(n, t):
-            banks = []
-            for u in range(HALVES):
-                bank = h_psum.tile([P, 2, CENTRES, P], F32, name="h_bank")
-                banks.append(bank)
-                tensor_banks[(n, t, u)] = bank
+        def tensor_squares(n, ts):
+            places = [(t, u) for t in ts for u in range(HALVES)]
+            for t, u in places:
+                tensor_banks[(n, t, u)] = h_psum.tile([P, 2, CENTRES, P], F32, name="h_bank")
 
-            def z_0(u, e):
+            def z_0(t, u, e):
                 return sq_tiles[n][:, e, t * WORDS + u * P : t * WORDS + (u + 1) * P]
 
             for e in range(2):
-                for u in range(HALVES):
+                for t, u in places:
+                    bank = tensor_banks[(n, t, u)]
                     if e == 0:
                         for both in range(2):
-                            nc.tensor.transpose(banks[u][:, both, 0, :], z_0(u, both), ident[:])
+                            nc.tensor.transpose(bank[:, both, 0, :], z_0(t, u, both), ident[:])
                     nc.tensor.matmul(
-                        out=banks[u][:, e, 1, :], lhsT=z_0(u, e), rhs=ident[:], start=True, stop=False, is_transpose=True
+                        out=bank[:, e, 1, :], lhsT=z_0(t, u, e), rhs=ident[:], start=True, stop=False, is_transpose=True
                     )
-                for u in range(HALVES):
+                for t, u in places:
                     first = t * HIDDEN + u * 2 * P + e
                     nc.tensor.matmul(
-                        out=banks[u][:, e, 1, :],
+                        out=tensor_banks[(n, t, u)][:, e, 1, :],
                         lhsT=h_raw_tiles[n][:, first : first + 2 * P - 1 : 2],
                         rhs=minus_four[:],
                         start=False,
@@ -200,7 +216,7 @@ def tile_kan1_pb_t_kernel(tc, h_mix, x, fc2_spline_w, fc2_base_w, fc2_base_b, ou
                     )
 
         with tc.tile_pool(name="w", bufs=PASSES) as w_pool, tc.tile_pool(
-            name="silu", bufs=6
+            name="silu", bufs=SILU_TILES
         ) as silu_pool, tc.psum_pool(name="w_bank", bufs=2) as w_psum:
             w_raw_tiles = {}
             w_bf_tiles = {}
@@ -219,20 +235,24 @@ def tile_kan1_pb_t_kernel(tc, h_mix, x, fc2_spline_w, fc2_base_w, fc2_base_b, ou
                 w_raw_tiles[s] = w_raw
 
             def silu(n):
-                silu_bf = silu_pool.tile([P, UNIT_H], BF16, name="silu_bf", align_bytes=64)
+                if n % SILU_GROUP == 0:
+                    silu_bf_tiles[n // SILU_GROUP] = silu_pool.tile(
+                        [P, SILU_GROUP, UNIT_H], BF16, name="silu_bf", align_bytes=64
+                    )
                 nc.scalar.activation(
-                    out=silu_bf[:].rearrange("p (w u e) -> p w u e", u=HALVES, e=2),
+                    out=silu_bf_tiles[n // SILU_GROUP][:, n % SILU_GROUP, :].rearrange(
+                        "p (w u e) -> p w u e", u=HALVES, e=2
+                    ),
                     in_=h_banks[(1, n)].rearrange("p (u w e) -> p w u e", u=HALVES, e=2),
                     func=ACT.Silu,
                 )
-                silu_bf_tiles[n] = silu_bf
 
-            def quantise_silu(n):
-                tokens = slice(n * UNIT, (n + 1) * UNIT)
+            def quantise_silu(group):
+                tokens = slice(group * SILU_GROUP * UNIT, (group + 1) * SILU_GROUP * UNIT)
                 nc.vector.quantize_mx(
                     out=silu_codes[:, tokens].bitcast(FP8X4),
                     scales=silu_scales[:, tokens],
-                    in_=silu_bf_tiles[n][:],
+                    in_=silu_bf_tiles[group][:].rearrange("p n c -> p (n c)"),
                 )
 
             def weight_words(s, m, half):
@@ -274,6 +294,8 @@ def tile_kan1_pb_t_kernel(tc, h_mix, x, fc2_spline_w, fc2_base_w, fc2_base_b, ou
 
             bias_rows = keep.tile([P, P], BF16)
             nc.vector.memset(bias_rows[:].bitcast(I32), 0)
+            vector_jobs = [n for n in range(UNITS) if is_vectors(n)]
+            tensor_jobs = [n for n in range(UNITS) if is_tensors(n)]
             for n in range(UNITS):
                 load_h(n)
                 if n == BANKS_AHEAD - 1:
@@ -292,18 +314,20 @@ def tile_kan1_pb_t_kernel(tc, h_mix, x, fc2_spline_w, fc2_base_w, fc2_base_b, ou
                 if n + BANKS_AHEAD < UNITS:
                     transpose_h(1, n + BANKS_AHEAD)
                 silu(n)
-                if n > 0:
-                    quantise_silu(n - 1)
-                if is_tensors(n) and n // TENSOR_EVERY < TENSOR_EARLY:
-                    tensor_square_0(n)
-                if n % VECTOR_STEP == VECTOR_FIRST and n // VECTOR_STEP < VECTOR_AHEAD:
-                    vector_squares(n // VECTOR_STEP * VECTOR_EVERY)
+                if n > 0 and n % SILU_GROUP == 0:
+                    quantise_silu(n // SILU_GROUP - 1)
+                if tensor_jobs and n >= tensor_jobs[0] and len(tensor_jobs) > TENSOR_LATE:
+                    tensor_square_0(tensor_jobs[0])
+                    tensor_jobs.remove(tensor_jobs[0])
+                if n % VECTOR_STEP == VECTOR_FIRST and n // VECTOR_STEP < VECTOR_TILES:
+                    vector_squares(vector_jobs[0])
+                    vector_jobs.remove(vector_jobs[0])
                 if n >= FIRST_LOT and (n - FIRST_LOT) % LOT_EVERY == 0:
                     s, pair = divmod((n - FIRST_LOT) // LOT_EVERY, 2)
                     if pair == 0 and s > 0:
                         quantise_weights(s - 1)
                     transpose_weights(2 * s + pair)
-            quantise_silu(UNITS - 1)
+            quantise_silu(UNITS // SILU_GROUP - 1)
             quantise_weights(PASSES - 1)
 
         with tc.tile_pool(name="basis", bufs=BASIS_TILES) as basis_pool, tc.tile_pool(
@@ -342,6 +366,66 @@ def tile_kan1_pb_t_kernel(tc, h_mix, x, fc2_spline_w, fc2_base_w, fc2_base_b, ou
                         scale=-0.25,
                     )
                 basis_bf_tiles[n] = basis_bf
+
+            def half_exponentials(half):
+                n = UNITS - 1
+                basis_bf = basis_pool.tile([P, UNIT_H // 2, CENTRES], BF16, name="basis_bf", align_bytes=64)
+                nc.scalar.activation(
+                    out=basis_bf[:].rearrange("p (u c) i -> p u c i", u=HALVES),
+                    in_=sq_tiles[n][:].rearrange("p i (u c) -> p u c i", u=HALVES)[:, :, half * 2 * P : (half + 1) * 2 * P, :],
+                    func=ACT.Exp,
+                    scale=-0.25,
+                )
+                basis_bf_tiles[(n, half)] = basis_bf
+
+            def half_quantise(half):
+                n = UNITS - 1
+                codes = basis_pool.tile([P, UNIT], U32, name="basis_codes", align_bytes=64)
+                scales = basis_pool.tile([P, UNIT], U8, name="basis_scales", align_bytes=64)
+                nc.vector.quantize_mx(
+                    out=codes[:].bitcast(FP8X4),
+                    scales=scales[:],
+                    in_=basis_bf_tiles[(n, half)][:].rearrange("p c i -> p (c i)"),
+                )
+                basis_mx_tiles[(n, half)] = (codes, scales)
+
+            def half_matmuls(half):
+                n = UNITS - 1
+                codes, scales = basis_mx_tiles[(n, half)]
+                tokens = slice(n * UNIT + half * P, n * UNIT + (half + 1) * P)
+                moving = [(silu_codes[:, tokens], silu_scales[:, tokens])]
+                for u in range(HALVES):
+                    moving.append((codes[:, u * P : (u + 1) * P], scales[:, u * P : (u + 1) * P]))
+                acc = acc_psum.tile([P, M_TILES, P], F32, name="acc")
+                for m in range(M_TILES):
+                    outputs = slice(m * P, (m + 1) * P)
+                    for s in range(PASSES):
+                        nc.tensor.matmul_mx(
+                            out=acc[:, m, :],
+                            lhsT=w_codes[:, s, outputs].bitcast(FP8X4),
+                            lhsT_scale=w_scales[:, s, outputs],
+                            rhs=moving[s][0].bitcast(FP8X4),
+                            rhs_scale=moving[s][1],
+                            start=(s == 0),
+                            stop=(s == PASSES - 1),
+                        )
+                acc_tiles[(n, half)] = acc
+
+            def half_finish(half):
+                b, piece = divmod(UNITS - 1, UNITS_PER_BATCH)
+                first = piece * UNIT + half * P
+                columns = slice(first, first + P)
+                out_sb = out_pool.tile([P, M_TILES, P], F32, name="out_sb")
+                for m in range(M_TILES):
+                    nc.vector.scalar_tensor_tensor(
+                        out=out_sb[:, m, :],
+                        in0=acc_tiles[(UNITS - 1, half)][:, m, :],
+                        scalar=bias[:, m : m + 1],
+                        in1=x_tiles[b][:, m, columns],
+                        op0=ALU.add,
+                        op1=ALU.add,
+                    )
+                nc.sync.dma_start(out=out[b, :, columns].rearrange("(m p) c -> p m c", p=P), in_=out_sb[:])
 
             def quantise_basis(n):
                 basis_codes = basis_pool.tile([P, HALVES * UNIT], U32, name="basis_codes", align_bytes=64)
@@ -399,27 +483,49 @@ def tile_kan1_pb_t_kernel(tc, h_mix, x, fc2_spline_w, fc2_base_w, fc2_base_b, ou
                 if piece == UNITS_PER_BATCH - 1 and b + X_TILES < BATCH:
                     load_x(b + X_TILES)
 
-            for n in range(-SQUARES_AHEAD - 1, UNITS + 2):
-                if is_scalars(n + SQUARES_AHEAD + 1):
-                    transpose_h(2, n + SQUARES_AHEAD + 1)
-                if is_tensors(n) and SPLIT_FILL:
-                    tensor_squares(n, 1)
-                if is_tensors(n + 1):
-                    tensor_squares(n + 1, 0)
-                    if not SPLIT_FILL:
-                        tensor_squares(n + 1, 1)
+            for n in range(-TR_AHEAD, UNITS + MM_LAG + FIN_LAG):
+                if is_scalars(n + TR_AHEAD):
+                    transpose_h(2, n + TR_AHEAD)
+                if GROUP == 2:
+                    if is_tensors(n + FILL_1):
+                        tensor_squares(n + FILL_1, [1])
+                    if is_tensors(n + FILL_0):
+                        tensor_squares(n + FILL_0, [0])
+                elif is_tensors(n + FILL_0):
+                    tensor_squares(n + FILL_0, [0, 1])
                 if is_scalars(n + SQUARES_AHEAD):
                     square_centre_0(n + SQUARES_AHEAD)
-                if 0 <= n < UNITS:
+                last = TAIL and n == UNITS - 1
+                if last:
+                    for half in range(2):
+                        half_exponentials(half)
+                elif 0 <= n < UNITS:
                     exponentials(n)
-                if 0 <= n - 1 < UNITS:
-                    quantise_basis(n - 1)
-                    matmuls(n - 1)
-                if 0 <= n - 2 < UNITS:
-                    finish(n - 2)
-                if is_scalars(n + SQUARES_AHEAD):
-                    square_centre_1(n + SQUARES_AHEAD)
-                if is_tensors(n + TENSOR_JOB) and (n + TENSOR_JOB) // TENSOR_EVERY >= TENSOR_EARLY:
-                    tensor_square_0(n + TENSOR_JOB)
-                if is_vectors(n) and is_vectors(n + VECTOR_EVERY * VECTOR_AHEAD):
-                    vector_squares(n + VECTOR_EVERY * VECTOR_AHEAD)
+                for what in ORDER:
+                    m = n - 1
+                    if what == "q" and 0 <= m < UNITS:
+                        if TAIL and m == UNITS - 1:
+                            half_quantise(0)
+                        else:
+                            quantise_basis(m)
+                    m = n - MM_LAG
+                    if what == "q" and 0 <= m < UNITS and not (TAIL and m == UNITS - 1):
+                        matmuls(m)
+                    if what == "q" and TAIL and m == UNITS - 1:
+                        half_matmuls(0)
+                    m = n - MM_LAG - FIN_LAG
+                    if what == "f" and 0 <= m < UNITS and not (TAIL and m == UNITS - 1):
+                        finish(m)
+                    if what == "f" and TAIL and n == UNITS:
+                        half_quantise(1)
+                        half_matmuls(1)
+                    if what == "f" and TAIL and m == UNITS - 1:
+                        half_finish(0)
+                        half_finish(1)
+                    if what == "s" and is_scalars(n + SQUARES_AHEAD):
+                        square_centre_1(n + SQUARES_AHEAD)
+                    if what == "u" and n + TENSOR_JOB in tensor_jobs:
+                        tensor_square_0(n + TENSOR_JOB)
+                    if what == "b" and is_vectors(n) and vector_jobs:
+                        vector_squares(vector_jobs[0])
+                        vector_jobs.remove(vector_jobs[0])

@@ -43,6 +43,8 @@ SQ_TILES = 3
 ROUND = "BUAA"
 TENSOR_LATE = 4
 GROUP = 2
+TWINS = 1
+ENDING = 1
 MERGE = 1
 VECTOR_TILES = 5
 SILU_GROUP = 2
@@ -50,10 +52,10 @@ SILU_TILES = 4
 TAIL = 0
 MM_LAG = 1
 FIN_LAG = 1
-FILL_0 = 1
-FILL_1 = 0
+FILL_0 = 2
+FILL_1 = 1
 ORDER = "qfsub"
-TR_AHEAD = 4
+TR_AHEAD = 5
 LOAD_W_EVERY = 6
 LOTS = 2 * PASSES
 FIRST_LOT = UNITS // 2
@@ -87,11 +89,7 @@ def is_scalars(n):
 def tile_kan1_pb_t_kernel(tc, h_mix, x, fc2_spline_w, fc2_base_w, fc2_base_b, out):
     nc = tc.nc
     with ExitStack() as stack:
-        stack.enter_context(
-            tc.manual_schedule(
-                engines={mybir.EngineType.Activation, mybir.EngineType.DVE, mybir.EngineType.Pool, mybir.EngineType.SP}
-            )
-        )
+        stack.enter_context(tc.manual_schedule())
         keep = stack.enter_context(tc.tile_pool(name="keep", bufs=1))
         h_raw_pool = stack.enter_context(tc.tile_pool(name="h_raw", bufs=UNITS))
         tensor_sq_pool = stack.enter_context(tc.tile_pool(name="tensor_sq", bufs=TENSOR_TILES))
@@ -476,16 +474,20 @@ def tile_kan1_pb_t_kernel(tc, h_mix, x, fc2_spline_w, fc2_base_w, fc2_base_b, ou
                             op0=ALU.add,
                             op1=ALU.add,
                         )
+                        if ENDING and n == UNITS - 1:
+                            nc.sync.dma_start(out=out[b, m * P : (m + 1) * P, columns], in_=out_sb[:, i, :])
                     rows = slice(2 * pair * P, 2 * (pair + 1) * P)
-                    nc.sync.dma_start(
-                        out=out[b, rows, columns].rearrange("(i p) c -> p i c", p=P), in_=out_sb[:]
-                    )
+                    if not (ENDING and n == UNITS - 1):
+                        nc.sync.dma_start(
+                            out=out[b, rows, columns].rearrange("(i p) c -> p i c", p=P), in_=out_sb[:]
+                        )
                 if piece == UNITS_PER_BATCH - 1 and b + X_TILES < BATCH:
                     load_x(b + X_TILES)
 
             for n in range(-TR_AHEAD, UNITS + MM_LAG + FIN_LAG):
-                if is_scalars(n + TR_AHEAD):
-                    transpose_h(2, n + TR_AHEAD)
+                for m in range(n + TR_AHEAD, n + TR_AHEAD + 2):
+                    if is_scalars(m) and (2, m) not in h_banks and (m == n + TR_AHEAD or TWINS and is_scalars(m - 1)):
+                        transpose_h(2, m)
                 if GROUP == 2:
                     if is_tensors(n + FILL_1):
                         tensor_squares(n + FILL_1, [1])

from contextlib import ExitStack

import concourse.mybir as mybir
from concourse.masks import make_identity

F32 = mybir.dt.float32
BF16 = mybir.dt.bfloat16
I32 = mybir.dt.int32
U32 = mybir.dt.uint32
U8 = mybir.dt.uint8
FP8X4 = mybir.dt.float8_e4m3fn_x4
ACT = mybir.ActivationFunctionType
ALU = mybir.AluOpType

P = 128
BATCH = 8
TOKENS = 768
HIDDEN = 512
OUTS = 512
M_TILES = OUTS // P
PACK = 4
K_PASS = P * PACK
PASSES = 3
HALVES = 2
CENTRES = 2
UNIT = 256
UNITS = BATCH * TOKENS // UNIT
UNITS_PER_BATCH = TOKENS // UNIT
UNIT_H = HALVES * UNIT * 2
WORDS = HIDDEN // 2
BANKS_AHEAD = 2
H_BANKS = 5
VECTOR_BANKS = 1
ACC_BANKS = 3
TENSOR_EVERY = 6
TENSOR_FIRST = 3
TENSOR_TILES = 3
TENSOR_JOB = 4
SPLIT_FILL = 1
BASIS_TILES = 3
OUT_TILES = 8
SQ_TILES = 3
ROUND = "BUAA"
TENSOR_LATE = 4
GROUP = 2
TWINS = 1
ENDING = 1
MERGE = 1
VECTOR_TILES = 5
SILU_GROUP = 2
SILU_TILES = 4
TAIL = 0
MM_LAG = 1
FIN_LAG = 1
FILL_0 = 2
FILL_1 = 1
ORDER = "qfsub"
TR_AHEAD = 5
LOAD_W_EVERY = 6
LOTS = 2 * PASSES
FIRST_LOT = UNITS // 2
LOT_EVERY = (UNITS - FIRST_LOT) // LOTS
X_TILES = 3
SQUARES_AHEAD = 3
VECTOR_EVERY = 4
VECTOR_AHEAD = 4
VECTOR_FIRST = 1
VECTOR_STEP = 4

FLOPS = 2 * BATCH * TOKENS * OUTS * (HIDDEN * CENTRES + HIDDEN)


def kind(n):
    return ROUND[n % len(ROUND)] if 0 <= n < UNITS else "none"


def is_vectors(n):
    return kind(n) == "B"


def is_tensors(n):
    return kind(n) == "U"


def is_scalars(n):
    return kind(n) == "A"


def tile_kan1_pb_t_kernel(tc, h_mix, x, fc2_spline_w, fc2_base_w, fc2_base_b, out):
    nc = tc.nc
    with ExitStack() as stack:
        stack.enter_context(tc.manual_schedule())
        keep = stack.enter_context(tc.tile_pool(name="keep", bufs=1))
        h_raw_pool = stack.enter_context(tc.tile_pool(name="h_raw", bufs=UNITS))
        tensor_sq_pool = stack.enter_context(tc.tile_pool(name="tensor_sq", bufs=TENSOR_TILES))
        x_pool = stack.enter_context(tc.tile_pool(name="x", bufs=X_TILES))
        sq_pool = stack.enter_context(tc.tile_pool(name="sq", bufs=SQ_TILES))
        vector_sq_pool = stack.enter_context(tc.tile_pool(name="vector_sq", bufs=VECTOR_TILES))
        h_sb_pool = stack.enter_context(tc.tile_pool(name="h_sb", bufs=2))
        h_psum = stack.enter_context(tc.psum_pool(name="h_bank", bufs=H_BANKS))
        vector_psum = h_psum if MERGE else stack.enter_context(tc.psum_pool(name="vector_bank", bufs=VECTOR_BANKS))

        ident = keep.tile([P, P], F32)
        make_identity(nc, ident[:])
        minus_four = keep.tile([P, P], BF16)
        nc.vector.tensor_scalar(
            out=minus_four[:], in0=ident[:], scalar1=-4.0, scalar2=0.0, op0=ALU.mult, op1=ALU.add
        )
        one = keep.tile([P, 1], F32)
        nc.vector.memset(one[:], 1.0)
        minus_quarter = keep.tile([P, 1], F32)
        nc.vector.memset(minus_quarter[:], -0.25)
        bias = keep.tile([P, M_TILES], F32)
        silu_codes = keep.tile([P, UNITS * UNIT], U32, align_bytes=64)
        silu_scales = keep.tile([P, UNITS * UNIT], U8, align_bytes=64)
        w_codes = keep.tile([P, PASSES, OUTS], U32, align_bytes=64)
        w_scales = keep.tile([P, PASSES, OUTS], U8, align_bytes=64)

        h_rows = h_mix.rearrange("b c j -> (b c) j")
        h_raw_tiles = {}
        h_banks = {}
        x_tiles = {}

        def load_h(n):
            h_raw = h_raw_pool.tile([P, (UNIT // P) * HIDDEN], BF16, name="h_raw")
            nc.sync.dma_start(
                out=h_raw[:].rearrange("r (t j) -> r t j", j=HIDDEN),
                in_=h_rows[n * UNIT : (n + 1) * UNIT, :].rearrange("(t r) j -> r t j", r=P),
            )
            h_raw_tiles[n] = h_raw

        def load_x(b):
            x_sb = x_pool.tile([P, M_TILES, TOKENS], BF16, name="x_sb")
            nc.sync.dma_start(out=x_sb[:], in_=x[b].rearrange("(m p) c -> p m c", p=P))
            x_tiles[b] = x_sb

        def transpose_h(phase, n, psum=h_psum):
            h_words = h_raw_tiles[n][:].bitcast(F32)
            h_bank = psum.tile([P, HALVES * UNIT], F32, name="h_bank")
            for t in range(UNIT // P):
                for u in range(HALVES):
                    nc.tensor.transpose(
                        h_bank[:, u * UNIT + t * P : u * UNIT + (t + 1) * P],
                        h_words[:, t * WORDS + u * P : t * WORDS + (u + 1) * P],
                        ident[:],
                    )
            h_banks[(phase, n)] = h_bank[:].bitcast(BF16)
            return h_bank

        sq_tiles = {}

        def square_centre_0(n):
            sq = sq_pool.tile([P, CENTRES, UNIT_H], F32, name="sq")
            nc.scalar.activation(out=sq[:, 0, :], in_=h_banks[(2, n)], func=ACT.Square, bias=one[:])
            sq_tiles[n] = sq

        def square_centre_1(n):
            sq = sq_tiles[n]
            nc.vector.scalar_tensor_tensor(
                out=sq[:, 1, :], in0=h_banks[(2, n)], scalar=-4.0, in1=sq[:, 0, :], op0=ALU.mult, op1=ALU.add
            )

        def vector_squares(n):
            h_bank = transpose_h(2, n, psum=vector_psum)
            h_sb = h_sb_pool.tile([P, HALVES * UNIT], F32, name="h_sb")
            nc.vector.tensor_copy(out=h_sb[:], in_=h_bank[:])
            sq = vector_sq_pool.tile([P, CENTRES, UNIT_H], F32, name="vector_sq")
            for i in range(CENTRES):
                nc.vector.scalar_tensor_tensor(
                    out=sq[:, i, :],
                    in0=h_banks[(2, n)],
                    scalar=2.0 - 4.0 * i,
                    in1=h_sb[:].bitcast(BF16),
                    op0=ALU.add,
                    op1=ALU.mult,
                )
            sq_tiles[n] = sq

        def tensor_square_0(n):
            sq = tensor_sq_pool.tile([P, 2, UNIT // P * WORDS], F32, name="tensor_sq")
            h = h_raw_tiles[n][:].rearrange("r (q e) -> r e q", e=2)
            nc.vector.scalar_tensor_tensor(
                out=sq[:], in0=h, scalar=2.0, in1=h, op0=ALU.add, op1=ALU.mult
            )
            sq_tiles[n] = sq

        tensor_banks = {}

        def tensor_squares(n, ts):
            places = [(t, u) for t in ts for u in range(HALVES)]
            for t, u in places:
                tensor_banks[(n, t, u)] = h_psum.tile([P, 2, CENTRES, P], F32, name="h_bank")

            def z_0(t, u, e):
                return sq_tiles[n][:, e, t * WORDS + u * P : t * WORDS + (u + 1) * P]

            for e in range(2):
                for t, u in places:
                    bank = tensor_banks[(n, t, u)]
                    if e == 0:
                        for both in range(2):
                            nc.tensor.transpose(bank[:, both, 0, :], z_0(t, u, both), ident[:])
                    nc.tensor.matmul(
                        out=bank[:, e, 1, :], lhsT=z_0(t, u, e), rhs=ident[:], start=True, stop=False, is_transpose=True
                    )
                for t, u in places:
                    first = t * HIDDEN + u * 2 * P + e
                    nc.tensor.matmul(
                        out=tensor_banks[(n, t, u)][:, e, 1, :],
                        lhsT=h_raw_tiles[n][:, first : first + 2 * P - 1 : 2],
                        rhs=minus_four[:],
                        start=False,
                        stop=True,
                    )

        with tc.tile_pool(name="w", bufs=PASSES) as w_pool, tc.tile_pool(
            name="silu", bufs=SILU_TILES
        ) as silu_pool, tc.psum_pool(name="w_bank", bufs=2) as w_psum:
            w_raw_tiles = {}
            w_bf_tiles = {}
            silu_bf_tiles = {}

            def load_weights(s):
                w_raw = w_pool.tile([P, M_TILES * K_PASS], BF16, name="w_raw")
                if s == 0:
                    columns = fc2_base_w
                else:
                    columns = fc2_spline_w[:, (s - 1) * K_PASS : s * K_PASS]
                nc.sync.dma_start(
                    out=w_raw[:].rearrange("r (m k) -> r m k", k=K_PASS),
                    in_=columns.rearrange("(m r) k -> r m k", r=P),
                )
                w_raw_tiles[s] = w_raw

            def silu(n):
                if n % SILU_GROUP == 0:
                    silu_bf_tiles[n // SILU_GROUP] = silu_pool.tile(
                        [P, SILU_GROUP, UNIT_H], BF16, name="silu_bf", align_bytes=64
                    )
                nc.scalar.activation(
                    out=silu_bf_tiles[n // SILU_GROUP][:, n % SILU_GROUP, :].rearrange(
                        "p (w u e) -> p w u e", u=HALVES, e=2
                    ),
                    in_=h_banks[(1, n)].rearrange("p (u w e) -> p w u e", u=HALVES, e=2),
                    func=ACT.Silu,
                )

            def quantise_silu(group):
                tokens = slice(group * SILU_GROUP * UNIT, (group + 1) * SILU_GROUP * UNIT)
                nc.vector.quantize_mx(
                    out=silu_codes[:, tokens].bitcast(FP8X4),
                    scales=silu_scales[:, tokens],
                    in_=silu_bf_tiles[group][:].rearrange("p n c -> p (n c)"),
                )

            def weight_words(s, m, half):
                words = w_raw_tiles[s][:].bitcast(F32)
                first = m * (K_PASS // 2)
                if s == 0:
                    return words[:, first + half * P : first + (half + 1) * P]
                return words[:, first + half : first + 2 * P : 2]

            def transpose_weights(lot):
                s, pair = divmod(lot, 2)
                if pair == 0:
                    w_bf_tiles[s] = w_pool.tile([P, OUTS * PACK], BF16, name="w_bf", align_bytes=64)
                w_bank = w_psum.tile([P, 2, 2, P], F32, name="w_bank")
                for i in range(2):
                    for half in range(2):
                        nc.tensor.transpose(
                            w_bank[:, i, half, :], weight_words(s, 2 * pair + i, half), ident[:]
                        )
                w_bf_words = w_bf_tiles[s][:].bitcast(F32)
                nc.vector.tensor_copy(
                    out=w_bf_words[:, 2 * pair * 2 * P : 2 * (pair + 1) * 2 * P].rearrange(
                        "p (i r half) -> p i r half", i=2, half=2
                    ),
                    in_=w_bank[:].rearrange("p i half r -> p i r half"),
                )

            def quantise_weights(s):
                nc.vector.quantize_mx(
                    out=w_codes[:, s, :].bitcast(FP8X4), scales=w_scales[:, s, :], in_=w_bf_tiles[s][:]
                )

            def transpose_bias():
                bias_rows_f32 = keep.tile([P, P], F32)
                nc.vector.tensor_copy(out=bias_rows_f32[:], in_=bias_rows[:])
                bias_bank = w_psum.tile([P, P], F32, name="bias_bank", tag="w_bank")
                nc.tensor.transpose(bias_bank[:], bias_rows_f32[:], ident[:])
                nc.vector.tensor_copy(out=bias[:], in_=bias_bank[:, 0:M_TILES])

            bias_rows = keep.tile([P, P], BF16)
            nc.vector.memset(bias_rows[:].bitcast(I32), 0)
            vector_jobs = [n for n in range(UNITS) if is_vectors(n)]
            tensor_jobs = [n for n in range(UNITS) if is_tensors(n)]
            for n in range(UNITS):
                load_h(n)
                if n == BANKS_AHEAD - 1:
                    nc.sync.dma_start(
                        out=bias_rows[0:M_TILES, :], in_=fc2_base_b.rearrange("(m p) -> m p", p=P)
                    )
                if n % LOAD_W_EVERY == 0 and 0 < n // LOAD_W_EVERY <= PASSES:
                    load_weights(n // LOAD_W_EVERY - 1)
            for b in range(X_TILES):
                load_x(b)

            for n in range(BANKS_AHEAD):
                transpose_h(1, n)
            transpose_bias()
            for n in range(UNITS):
                if n + BANKS_AHEAD < UNITS:
                    transpose_h(1, n + BANKS_AHEAD)
                silu(n)
                if n > 0 and n % SILU_GROUP == 0:
                    quantise_silu(n // SILU_GROUP - 1)
                if tensor_jobs and n >= tensor_jobs[0] and len(tensor_jobs) > TENSOR_LATE:
                    tensor_square_0(tensor_jobs[0])
                    tensor_jobs.remove(tensor_jobs[0])
                if n % VECTOR_STEP == VECTOR_FIRST and n // VECTOR_STEP < VECTOR_TILES:
                    vector_squares(vector_jobs[0])
                    vector_jobs.remove(vector_jobs[0])
                if n >= FIRST_LOT and (n - FIRST_LOT) % LOT_EVERY == 0:
                    s, pair = divmod((n - FIRST_LOT) // LOT_EVERY, 2)
                    if pair == 0 and s > 0:
                        quantise_weights(s - 1)
                    transpose_weights(2 * s + pair)
            quantise_silu(UNITS // SILU_GROUP - 1)
            quantise_weights(PASSES - 1)

        with tc.tile_pool(name="basis", bufs=BASIS_TILES) as basis_pool, tc.tile_pool(
            name="out", bufs=OUT_TILES
        ) as out_pool, tc.psum_pool(name="acc", bufs=ACC_BANKS) as acc_psum:
            basis_bf_tiles = {}
            basis_mx_tiles = {}
            acc_tiles = {}

            def exponentials(n):
                basis_bf = basis_pool.tile([P, UNIT_H, CENTRES], BF16, name="basis_bf", align_bytes=64)
                if is_tensors(n):
                    for t in range(UNIT // P):
                        for u in range(HALVES):
                            first = (u * UNIT + t * P) * 2
                            nc.scalar.activation(
                                out=basis_bf[:, first : first + 2 * P, :].rearrange("p (w e) i -> p w (e i)", e=2),
                                in_=tensor_banks[(n, t, u)][:].rearrange("p e i w -> p w (e i)"),
                                func=ACT.Exp,
                                scale=-0.25,
                                bias=minus_quarter[:],
                            )
                elif is_vectors(n):
                    nc.scalar.activation(
                        out=basis_bf[:],
                        in_=sq_tiles[n][:].rearrange("p i c -> p c i"),
                        func=ACT.Exp,
                        scale=-0.25,
                        bias=minus_quarter[:],
                    )
                else:
                    nc.scalar.activation(
                        out=basis_bf[:],
                        in_=sq_tiles[n][:].rearrange("p i c -> p c i"),
                        func=ACT.Exp,
                        scale=-0.25,
                    )
                basis_bf_tiles[n] = basis_bf

            def half_exponentials(half):
                n = UNITS - 1
                basis_bf = basis_pool.tile([P, UNIT_H // 2, CENTRES], BF16, name="basis_bf", align_bytes=64)
                nc.scalar.activation(
                    out=basis_bf[:].rearrange("p (u c) i -> p u c i", u=HALVES),
                    in_=sq_tiles[n][:].rearrange("p i (u c) -> p u c i", u=HALVES)[:, :, half * 2 * P : (half + 1) * 2 * P, :],
                    func=ACT.Exp,
                    scale=-0.25,
                )
                basis_bf_tiles[(n, half)] = basis_bf

            def half_quantise(half):
                n = UNITS - 1
                codes = basis_pool.tile([P, UNIT], U32, name="basis_codes", align_bytes=64)
                scales = basis_pool.tile([P, UNIT], U8, name="basis_scales", align_bytes=64)
                nc.vector.quantize_mx(
                    out=codes[:].bitcast(FP8X4),
                    scales=scales[:],
                    in_=basis_bf_tiles[(n, half)][:].rearrange("p c i -> p (c i)"),
                )
                basis_mx_tiles[(n, half)] = (codes, scales)

            def half_matmuls(half):
                n = UNITS - 1
                codes, scales = basis_mx_tiles[(n, half)]
                tokens = slice(n * UNIT + half * P, n * UNIT + (half + 1) * P)
                moving = [(silu_codes[:, tokens], silu_scales[:, tokens])]
                for u in range(HALVES):
                    moving.append((codes[:, u * P : (u + 1) * P], scales[:, u * P : (u + 1) * P]))
                acc = acc_psum.tile([P, M_TILES, P], F32, name="acc")
                for m in range(M_TILES):
                    outputs = slice(m * P, (m + 1) * P)
                    for s in range(PASSES):
                        nc.tensor.matmul_mx(
                            out=acc[:, m, :],
                            lhsT=w_codes[:, s, outputs].bitcast(FP8X4),
                            lhsT_scale=w_scales[:, s, outputs],
                            rhs=moving[s][0].bitcast(FP8X4),
                            rhs_scale=moving[s][1],
                            start=(s == 0),
                            stop=(s == PASSES - 1),
                        )
                acc_tiles[(n, half)] = acc

            def half_finish(half):
                b, piece = divmod(UNITS - 1, UNITS_PER_BATCH)
                first = piece * UNIT + half * P
                columns = slice(first, first + P)
                out_sb = out_pool.tile([P, M_TILES, P], F32, name="out_sb")
                for m in range(M_TILES):
                    nc.vector.scalar_tensor_tensor(
                        out=out_sb[:, m, :],
                        in0=acc_tiles[(UNITS - 1, half)][:, m, :],
                        scalar=bias[:, m : m + 1],
                        in1=x_tiles[b][:, m, columns],
                        op0=ALU.add,
                        op1=ALU.add,
                    )
                nc.sync.dma_start(out=out[b, :, columns].rearrange("(m p) c -> p m c", p=P), in_=out_sb[:])

            def quantise_basis(n):
                basis_codes = basis_pool.tile([P, HALVES * UNIT], U32, name="basis_codes", align_bytes=64)
                basis_scales = basis_pool.tile([P, HALVES * UNIT], U8, name="basis_scales", align_bytes=64)
                nc.vector.quantize_mx(
                    out=basis_codes[:].bitcast(FP8X4),
                    scales=basis_scales[:],
                    in_=basis_bf_tiles[n][:].rearrange("p c i -> p (c i)"),
                )
                basis_mx_tiles[n] = (basis_codes, basis_scales)

            def matmuls(n):
                basis_codes, basis_scales = basis_mx_tiles[n]
                tokens = slice(n * UNIT, (n + 1) * UNIT)
                moving = [(silu_codes[:, tokens], silu_scales[:, tokens])]
                for u in range(HALVES):
                    words = slice(u * UNIT, (u + 1) * UNIT)
                    moving.append((basis_codes[:, words], basis_scales[:, words]))
                for pair in range(M_TILES // 2):
                    acc = acc_psum.tile([P, 2, UNIT], F32, name="acc")
                    for i in range(2):
                        outputs = slice((2 * pair + i) * P, (2 * pair + i + 1) * P)
                        for s in range(PASSES):
                            codes, scales = moving[s]
                            nc.tensor.matmul_mx(
                                out=acc[:, i, :],
                                lhsT=w_codes[:, s, outputs].bitcast(FP8X4),
                                lhsT_scale=w_scales[:, s, outputs],
                                rhs=codes.bitcast(FP8X4),
                                rhs_scale=scales,
                                start=(s == 0),
                                stop=(s == PASSES - 1),
                            )
                    acc_tiles[(n, pair)] = acc

            def finish(n):
                b, piece = divmod(n, UNITS_PER_BATCH)
                columns = slice(piece * UNIT, (piece + 1) * UNIT)
                for pair in range(M_TILES // 2):
                    out_sb = out_pool.tile([P, 2, UNIT], F32, name="out_sb")
                    for i in range(2):
                        m = 2 * pair + i
                        nc.vector.scalar_tensor_tensor(
                            out=out_sb[:, i, :],
                            in0=acc_tiles[(n, pair)][:, i, :],
                            scalar=bias[:, m : m + 1],
                            in1=x_tiles[b][:, m, columns],
                            op0=ALU.add,
                            op1=ALU.add,
                        )
                        if ENDING and n == UNITS - 1:
                            nc.sync.dma_start(out=out[b, m * P : (m + 1) * P, columns], in_=out_sb[:, i, :])
                    rows = slice(2 * pair * P, 2 * (pair + 1) * P)
                    if not (ENDING and n == UNITS - 1):
                        nc.sync.dma_start(
                            out=out[b, rows, columns].rearrange("(i p) c -> p i c", p=P), in_=out_sb[:]
                        )
                if piece == UNITS_PER_BATCH - 1 and b + X_TILES < BATCH:
                    load_x(b + X_TILES)

            for n in range(-TR_AHEAD, UNITS + MM_LAG + FIN_LAG):
                for m in range(n + TR_AHEAD, n + TR_AHEAD + 2):
                    if is_scalars(m) and (2, m) not in h_banks and (m == n + TR_AHEAD or TWINS and is_scalars(m - 1)):
                        transpose_h(2, m)
                if GROUP == 2:
                    if is_tensors(n + FILL_1):
                        tensor_squares(n + FILL_1, [1])
                    if is_tensors(n + FILL_0):
                        tensor_squares(n + FILL_0, [0])
                elif is_tensors(n + FILL_0):
                    tensor_squares(n + FILL_0, [0, 1])
                if is_scalars(n + SQUARES_AHEAD):
                    square_centre_0(n + SQUARES_AHEAD)
                last = TAIL and n == UNITS - 1
                if last:
                    for half in range(2):
                        half_exponentials(half)
                elif 0 <= n < UNITS:
                    exponentials(n)
                for what in ORDER:
                    m = n - 1
                    if what == "q" and 0 <= m < UNITS:
                        if TAIL and m == UNITS - 1:
                            half_quantise(0)
                        else:
                            quantise_basis(m)
                    m = n - MM_LAG
                    if what == "q" and 0 <= m < UNITS and not (TAIL and m == UNITS - 1):
                        matmuls(m)
                    if what == "q" and TAIL and m == UNITS - 1:
                        half_matmuls(0)
                    m = n - MM_LAG - FIN_LAG
                    if what == "f" and 0 <= m < UNITS and not (TAIL and m == UNITS - 1):
                        finish(m)
                    if what == "f" and TAIL and n == UNITS:
                        half_quantise(1)
                        half_matmuls(1)
                    if what == "f" and TAIL and m == UNITS - 1:
                        half_finish(0)
                        half_finish(1)
                    if what == "s" and is_scalars(n + SQUARES_AHEAD):
                        square_centre_1(n + SQUARES_AHEAD)
                    if what == "u" and n + TENSOR_JOB in tensor_jobs:
                        tensor_square_0(n + TENSOR_JOB)
                    if what == "b" and is_vectors(n) and vector_jobs:
                        vector_squares(vector_jobs[0])
                        vector_jobs.remove(vector_jobs[0])
